import numpy as np
import ml_dtypes


def mxq(x, axis, fmt="e4m3"):
    dtype, down = {"e4m3": (ml_dtypes.float8_e4m3fn, 7), "e5m2": (ml_dtypes.float8_e5m2, 14)}[fmt]
    v = np.moveaxis(np.asarray(x, np.float32).astype(ml_dtypes.bfloat16).astype(np.float64), axis, -1)
    blocks = v.reshape(v.shape[:-1] + (-1, 32))
    amax = np.abs(blocks).max(-1, keepdims=True)
    byte = np.maximum(np.where(amax > 0, np.frexp(amax)[1] - 1 + 127, 0) - down, 1)
    scale = np.exp2(byte - 127.0)
    codes = (blocks / scale).astype(np.float32).astype(dtype).astype(np.float64)
    return np.moveaxis((codes * scale).reshape(v.shape), -1, axis)


WIDE = False


def mx_kscale(k):
    if not WIDE:
        return np.ones(k)
    levels = np.array([10, -10, 5, -5, 0])
    a = np.random.permutation(np.resize(levels, k // 512 * 4)).reshape(k // 512, 4)
    idx = np.arange(k)
    return np.exp2(a[idx // 512, idx % 128 // 32])


BF16 = ml_dtypes.bfloat16


def bf(x):
    return np.asarray(x, np.float32).astype(BF16)


def f64(x):
    return np.asarray(x).astype(np.float64)


B, C, T, TF, CCONF, GROUPS = 48, 512, 64, 256, 512, 32
EPS = 1e-5


def group_norm(x, gamma, beta):
    b_, c_, t_ = x.shape
    xg = x.reshape(b_, GROUPS, c_ // GROUPS, t_)
    mu = xg.mean(axis=(2, 3), keepdims=True)
    var = xg.var(axis=(2, 3), keepdims=True)
    xg = (xg - mu) / np.sqrt(var + EPS)
    return xg.reshape(b_, c_, t_) * gamma[None, :, None] + beta[None, :, None]


def pool(fh, lo, hi):
    idx = np.arange(fh.shape[-1])
    out = np.empty((fh.shape[0], fh.shape[1], lo.shape[1]))
    for i in range(fh.shape[0]):
        mask = (idx[None, :] > lo[i][:, None] - 1.0) & (idx[None, :] <= hi[i][:, None])
        out[i] = np.where(mask[None, :, :], fh[i][:, None, :], -np.inf).max(-1)
    return np.where(np.isfinite(out), out, 0.0)


def boundary_max_pooling(feature, segments):
    tin = feature.shape[-1]
    half = feature.shape[1] // 2
    s = np.clip(segments, 0.0, tin - 1.0)
    left = pool(feature[:, :half], s[..., 0], s[..., 1])
    right = pool(feature[:, half:], s[..., 2], s[..., 3])
    return np.concatenate([left, right], axis=1)


def make_segments(n, tin):
    lo = np.random.uniform(size=(B, n, 2)) * (1.25 * tin) - 0.125 * tin
    ln = np.random.uniform(size=(B, n, 2)) * (tin / 4) + 1.0
    ln = np.where(np.random.uniform(size=(B, n, 2)) < 0.1, -ln, ln)
    hi = lo + ln
    return np.stack([lo[..., 0], hi[..., 0], lo[..., 1], hi[..., 1]], axis=-1)


def setup_inputs():
    s = mx_kscale(C)
    return {
        'frame_level_feature': bf(np.random.standard_normal((B, C, TF)) * s[None, :, None]),
        'frame_segments': bf(make_segments(T, TF)),
        'w_roi': bf(np.random.standard_normal((C, C)) * 0.5 * C ** -0.5 / s[None, :]),
        'b_roi': bf(np.random.standard_normal(C) * 0.3),
        'g_roi': bf(1.0 + 0.2 * np.random.standard_normal(C)),
        'be_roi': bf(np.random.standard_normal(C) * 0.3),
    }


def reference(frame_level_feature, frame_segments, w_roi, b_roi, g_roi, be_roi):
    pooled = boundary_max_pooling(f64(frame_level_feature), f64(frame_segments))
    y = (mxq(f64(w_roi), 1, 'e4m3') @ mxq(pooled, 1, 'e4m3')) + f64(b_roi)[None, :, None]
    return np.maximum(group_norm(y, f64(g_roi), f64(be_roi)), 0.0)

@@ -1,0 +1,409 @@
+from contextlib import ExitStack
+
+import concourse.bass as bass
+import concourse.mybir as mybir
+from concourse.masks import make_identity
+
+F32 = mybir.dt.float32
+BF16 = mybir.dt.bfloat16
+I32 = mybir.dt.int32
+U32 = mybir.dt.uint32
+U8 = mybir.dt.uint8
+FP8X4 = mybir.dt.float8_e4m3fn_x4
+ALU = mybir.AluOpType
+ACT = mybir.ActivationFunctionType
+AX = mybir.AxisListType
+
+P = 128
+NB = 48
+NT = 256
+NN = 64
+LEVELS = 8
+GB = 8
+SLOTS = 3
+SLOT_ROWS = 4096
+SLOT_WORDS = SLOT_ROWS * P
+EPS = 1e-5
+
+FLOPS = 2 * 48 * 512 * 512 * 64
+
+
+def level_cols(k):
+    if k == 0:
+        return NT
+    if k == 1:
+        return NT - 1
+    return NT + 2 - 2 ** k
+
+
+def tile_coarsepyramid_pb_kernel(
+    tc, frame_level_feature, frame_segments, w_roi, b_roi, g_roi, be_roi, out
+):
+    nc = tc.nc
+    with ExitStack() as ctx:
+        keep = ctx.enter_context(tc.tile_pool(name="keep", bufs=1))
+        stage = ctx.enter_context(tc.tile_pool(name="stage", bufs=3))
+        gat = ctx.enter_context(tc.tile_pool(name="gat", bufs=4))
+        grpp = ctx.enter_context(tc.tile_pool(name="grpp", bufs=2))
+        small = ctx.enter_context(tc.tile_pool(name="small", bufs=2))
+        psum = ctx.enter_context(tc.psum_pool(name="psum", bufs=1))
+
+        out_flat = out.rearrange("b c n -> (b c n)")
+        out_rows = out_flat.rearrange("(r w) -> r w", w=P)
+        out_final = out.rearrange("b (m j) n -> m b (j n)", j=4)
+
+        one = keep.tile([P, 1], F32, name="one")
+        nc.vector.memset(one[:], 1.0)
+        one2 = keep.tile([P, 1], F32, name="one2")
+        nc.scalar.activation(out=one2[:], in_=one[:], func=ACT.Sqrt)
+
+        ident_f = keep.tile([P, P], F32, name="ident_f")
+        make_identity(nc, ident_f[:])
+        ident_b = keep.tile([P, P], BF16, name="ident_b")
+        make_identity(nc, ident_b[:])
+
+        segb = keep.tile([P, 4 * NN], BF16, name="segb")
+        nc.vector.memset(segb[:], 0.0)
+        nc.sync.dma_start(out=segb[0:NB, :], in_=frame_segments.rearrange("b n f -> b (n f)"))
+
+        tabs = []
+        for i in range(SLOTS):
+            tabs.append(keep.tile([P, 2, LEVELS, 2, NT], BF16, name="tab%d" % i))
+
+        def load(b):
+            nc.sync.dma_start(
+                out=tabs[b % SLOTS][:, :, 0, :, :],
+                in_=frame_level_feature[b].rearrange("(s p e) t -> p s e t", s=2, e=2),
+            )
+
+        load(0)
+
+        w_sb = keep.tile([P, 4, 512], BF16, name="w_sb")
+        nc.sync.dma_start(out=w_sb[:], in_=w_roi.rearrange("(m j) c -> m j c", j=4))
+        pb_b = keep.tile([P, 4], BF16, name="pb_b")
+        nc.sync.dma_start(out=pb_b[:], in_=b_roi.rearrange("(m j) -> m j", j=4))
+        pb_g = keep.tile([P, 4], BF16, name="pb_g")
+        nc.sync.dma_start(out=pb_g[:], in_=g_roi.rearrange("(m j) -> m j", j=4))
+        pb_e = keep.tile([P, 4], BF16, name="pb_e")
+        nc.sync.dma_start(out=pb_e[:], in_=be_roi.rearrange("(m j) -> m j", j=4))
+
+        for i in range(SLOTS):
+            for k in range(1, LEVELS):
+                nc.vector.memset(tabs[i][:, :, k, :, level_cols(k):NT], 0.0)
+
+        W2 = 2 * NN
+        sf = keep.tile([P, 2 * W2], F32, name="sf")
+        nc.vector.tensor_scalar(
+            out=sf[:], in0=segb[:], scalar1=0.0, scalar2=float(NT - 1), op0=ALU.max, op1=ALU.min
+        )
+        si = keep.tile([P, 2 * W2], I32, name="si")
+        nc.vector.tensor_copy(out=si[:], in_=sf[:])
+        fi = keep.tile([P, 2 * W2], F32, name="fi")
+        nc.vector.tensor_copy(out=fi[:], in_=si[:])
+        gt = keep.tile([P, 2 * W2], F32, name="gt")
+        nc.vector.tensor_tensor(out=gt[:], in0=fi[:], in1=sf[:], op=ALU.is_gt)
+        fl = keep.tile([P, 2 * W2], F32, name="fl")
+        nc.vector.tensor_sub(out=fl[:], in0=fi[:], in1=gt[:])
+        fl2 = fl[:].rearrange("p (w e) -> p w e", e=2)
+        lo = fl2[:, :, 0]
+        hi = fl2[:, :, 1]
+
+        ld = keep.tile([P, W2], F32, name="ld")
+        nc.vector.tensor_sub(out=ld[:], in0=hi, in1=lo)
+        ne = keep.tile([P, W2], F32, name="ne")
+        nc.vector.tensor_single_scalar(out=ne[:], in_=ld[:], scalar=0.0, op=ALU.is_ge)
+        lc = keep.tile([P, W2], F32, name="lc")
+        nc.vector.tensor_scalar(
+            out=lc[:], in0=ld[:], scalar1=0.0, scalar2=1.0, op0=ALU.max, op1=ALU.add
+        )
+        s2i = keep.tile([P, W2], I32, name="s2i")
+        nc.vector.tensor_single_scalar(
+            out=s2i[:], in_=lc[:].bitcast(I32), scalar=0x7F800000, op=ALU.bitwise_and
+        )
+        kei = keep.tile([P, W2], I32, name="kei")
+        nc.vector.tensor_single_scalar(
+            out=kei[:], in_=lc[:].bitcast(I32), scalar=23, op=ALU.logical_shift_right
+        )
+        kf = keep.tile([P, W2], F32, name="kf")
+        nc.vector.tensor_copy(out=kf[:], in_=kei[:])
+        kk = keep.tile([P, W2], F32, name="kk")
+        nc.vector.tensor_scalar(
+            out=kk[:], in0=kf[:], scalar1=-127.0, scalar2=float(LEVELS - 1), op0=ALU.add, op1=ALU.min
+        )
+        s2 = keep.tile([P, W2], F32, name="s2")
+        nc.vector.tensor_scalar_min(out=s2[:], in0=s2i[:].bitcast(F32), scalar1=128.0)
+        tb0 = keep.tile([P, W2], F32, name="tb0")
+        nc.vector.tensor_sub(out=tb0[:], in0=hi, in1=s2[:])
+        tbb = keep.tile([P, W2], F32, name="tbb")
+        nc.vector.tensor_scalar_add(out=tbb[:], in0=tb0[:], scalar1=1.0)
+
+        st_i = keep.tile([P, W2], I32, name="st_i")
+        nc.gpsimd.iota(st_i[:], pattern=[[0, NN], [1, 2]], base=0, channel_multiplier=0)
+        st_f = keep.tile([P, W2], F32, name="st_f")
+        nc.vector.tensor_copy(out=st_f[:], in_=st_i[:])
+
+        idx_f = []
+        for a, (t_ap, zbase) in enumerate(((lo, 94), (tbb[:], 2078))):
+            z_i = keep.tile([P, W2], I32, name="z_i%d" % a)
+            nc.gpsimd.iota(z_i[:], pattern=[[32, NN], [1, 2]], base=zbase, channel_multiplier=0)
+            z_f = keep.tile([P, W2], F32, name="z_f%d" % a)
+            nc.vector.tensor_copy(out=z_f[:], in_=z_i[:])
+            g1 = keep.tile([P, W2], F32, name="g1_%d" % a)
+            nc.vector.tensor_scalar(
+                out=g1[:], in0=t_ap, scalar1=128.0, scalar2=-4094.0, op0=ALU.is_ge, op1=ALU.mult
+            )
+            r1 = keep.tile([P, W2], F32, name="r1_%d" % a)
+            nc.vector.scalar_tensor_tensor(
+                out=r1[:], in0=t_ap, scalar=32.0, in1=g1[:], op0=ALU.mult, op1=ALU.add
+            )
+            r2 = keep.tile([P, W2], F32, name="r2_%d" % a)
+            nc.vector.scalar_tensor_tensor(
+                out=r2[:], in0=kk[:], scalar=4.0, in1=r1[:], op0=ALU.mult, op1=ALU.add
+            )
+            r3 = keep.tile([P, W2], F32, name="r3_%d" % a)
+            nc.vector.tensor_add(out=r3[:], in0=r2[:], in1=st_f[:])
+            r4 = keep.tile([P, W2], F32, name="r4_%d" % a)
+            nc.vector.tensor_sub(out=r4[:], in0=r3[:], in1=z_f[:])
+            r5 = keep.tile([P, W2], F32, name="r5_%d" % a)
+            nc.vector.tensor_mul(out=r5[:], in0=r4[:], in1=ne[:])
+            r6 = keep.tile([P, W2], F32, name="r6_%d" % a)
+            nc.vector.tensor_add(out=r6[:], in0=r5[:], in1=z_f[:])
+            idx_f.append(r6)
+
+        pidx = psum.tile([P, 2, P], F32, tag="tp", bufs=2, name="pidx")
+        for a in range(2):
+            nc.tensor.transpose(pidx[:, a, :], idx_f[a][:], ident_f[:])
+        idx_i = keep.tile([P, 2, NB], I32, name="idx_i")
+        for j in range(SLOTS):
+            nc.vector.tensor_scalar(
+                out=idx_i[:, :, j:NB:SLOTS],
+                in0=pidx[:, :, j:NB:SLOTS],
+                scalar1=float(SLOT_ROWS * j),
+                scalar2=None,
+                op0=ALU.add,
+            )
+
+        wg = keep.tile([P, 4, P, 4], BF16, name="wg", align_bytes=64)
+        wg_f = (
+            wg[:]
+            .rearrange("p j m t -> p (j m t)")
+            .bitcast(F32)
+            .rearrange("p (j m u) -> p j m u", j=4, u=2)
+        )
+        for jj in range(2):
+            pw = psum.tile([P, 2, 2, P], F32, tag="tp", bufs=2, name="pw")
+            for jl in range(2):
+                w_words = w_sb[:, 2 * jj + jl, :].bitcast(F32)
+                for u in range(2):
+                    nc.tensor.transpose(pw[:, jl, u, :], w_words[:, P * u:P * u + P], ident_f[:])
+            nc.vector.tensor_copy(
+                out=wg_f[:, 2 * jj:2 * jj + 2, :, :], in_=pw[:].rearrange("p j u m -> p j m u")
+            )
+        wq = keep.tile([P, 512], U32, name="wq", align_bytes=64)
+        ws = keep.tile([P, 512], U8, name="ws", align_bytes=64)
+        nc.vector.quantize_mx(
+            out=wq[:].bitcast(FP8X4), scales=ws[:], in_=wg[:].rearrange("p j m t -> p (j m t)")
+        )
+
+        beta = keep.tile([P, 4], F32, name="beta")
+        nc.vector.tensor_copy(out=beta[:], in_=pb_b[:])
+        gam = keep.tile([P, 4], F32, name="gam")
+        nc.vector.tensor_copy(out=gam[:], in_=pb_g[:])
+        bet2 = keep.tile([P, 4], F32, name="bet2")
+        nc.vector.tensor_copy(out=bet2[:], in_=pb_e[:])
+        beta64 = keep.tile([P, 4], F32, name="beta64")
+        nc.vector.tensor_scalar_mul(out=beta64[:], in0=beta[:], scalar1=float(NN))
+
+        gsum = keep.tile([P, 32], F32, name="gsum")
+        nc.vector.tensor_reduce(
+            out=gsum[:], in_=ident_f[:].rearrange("p (g d) -> p g d", d=4), axis=AX.X, op=ALU.add
+        )
+        bd = keep.tile([P, 32, 4], F32, name="bd")
+        nc.vector.tensor_scalar(
+            out=bd[:],
+            in0=gsum[:].unsqueeze(2).to_broadcast([P, 32, 4]),
+            scalar1=1.0 / 1024.0,
+            scalar2=None,
+            op0=ALU.mult,
+        )
+
+        res = keep.tile([P, NB, 4, NN], F32, name="res")
+
+        def tables(b):
+            t = tabs[b % SLOTS]
+            for k in range(1, LEVELS):
+                sh = 2 ** (k - 1)
+                n = level_cols(k)
+                nc.vector.tensor_tensor(
+                    out=t[:, :, k, :, 0:n],
+                    in0=t[:, :, k - 1, :, 0:n],
+                    in1=t[:, :, k - 1, :, sh:sh + n],
+                    op=ALU.max,
+                )
+
+        def flip_store(b):
+            t = tabs[b % SLOTS]
+            stg = stage.tile([P, LEVELS, 2, 2, 2, P], BF16, tag="stg", name="stg")
+            for k in range(LEVELS):
+                pt = psum.tile([P, 2, 2, 2, P], BF16, tag="tp", bufs=2, name="pt")
+                for h in range(2):
+                    for s in range(2):
+                        for e in range(2):
+                            nc.tensor.transpose(
+                                pt[:, h, s, e, :], t[:, s, k, e, P * h:P * h + P], ident_b[:]
+                            )
+                nc.scalar.copy(out=stg[:, k, :, :, :, :], in_=pt[:])
+            slot = b % SLOTS
+            nc.scalar.dma_start(
+                out=out_flat[slot * SLOT_WORDS:(slot + 1) * SLOT_WORDS].rearrange(
+                    "(p w) -> p w", p=P
+                ),
+                in_=stg[:].rearrange("p k h s e c -> p (k h s e c)").bitcast(F32),
+            )
+
+        gathered = {}
+
+        def gather(b):
+            pair = []
+            for a in range(2):
+                g = gat.tile([P, 2 * P], BF16, tag="g%d" % a, name="g%d" % a)
+                nc.gpsimd.indirect_dma_start(
+                    out=g[:].bitcast(F32),
+                    out_offset=None,
+                    in_=out_rows[0:(b % SLOTS + 1) * SLOT_ROWS, :],
+                    in_offset=bass.IndirectOffsetOnAxis(ap=idx_i[:, a, b:b + 1], axis=0),
+                )
+                pair.append(g)
+            gathered[b] = pair
+
+        groups = {}
+
+        def finish(b):
+            ga, gb = gathered[b]
+            pm = gat.tile([P, 2 * P], BF16, tag="pm", name="pm")
+            nc.vector.tensor_tensor(out=pm[:], in0=ga[:], in1=gb[:], op=ALU.max)
+            pp = psum.tile([P, 2, P], BF16, tag="pp", name="pp")
+            for e in range(2):
+                nc.tensor.transpose(pp[:, e, :], pm[:, P * e:P * e + P], ident_b[:])
+            if b % GB == 0:
+                groups[b // GB] = grpp.tile(
+                    [P, GB, NN, 4], BF16, tag="grp", name="grp", align_bytes=64
+                )
+            grp = groups[b // GB]
+            nc.scalar.copy(
+                out=grp[:, b % GB, :, :].rearrange("p n (s e) -> p n s e", e=2),
+                in_=pp[:].rearrange("p e (n s) -> p n s e", s=2),
+            )
+
+        def conv_norm(g):
+            grp = groups[g]
+            codes = grpp.tile([P, 512], U32, tag="codes", name="codes", align_bytes=64)
+            scl = grpp.tile([P, 512], U8, tag="scl", name="scl", align_bytes=64)
+            nc.vector.quantize_mx(
+                out=codes[:].bitcast(FP8X4),
+                scales=scl[:],
+                in_=grp[:].rearrange("p b n t -> p (b n t)"),
+            )
+            ys = []
+            for j in range(4):
+                y = psum.tile([P, GB, NN], F32, tag="y%d" % j, name="y%d" % j)
+                nc.tensor.matmul_mx(
+                    out=y[:].rearrange("p b n -> p (b n)"),
+                    lhsT=wq[:, P * j:P * j + P].bitcast(FP8X4),
+                    lhsT_scale=ws[:, P * j:P * j + P],
+                    rhs=codes[:].bitcast(FP8X4),
+                    rhs_scale=scl[:],
+                    start=True,
+                    stop=True,
+                )
+                ys.append(y)
+            st = small.tile([P, 2, 4, GB], F32, tag="st", name="st")
+            for j in range(4):
+                nc.vector.tensor_reduce(out=st[:, 0, j, :], in_=ys[j][:], axis=AX.X, op=ALU.add)
+                sq = small.tile([P, GB, NN], F32, tag="sq", name="sq")
+                nc.scalar.activation(
+                    out=sq[:], in_=ys[j][:], func=ACT.Square, bias=beta[:, j:j + 1], scale=1.0
+                )
+                nc.vector.tensor_reduce(out=st[:, 1, j, :], in_=sq[:], axis=AX.X, op=ALU.add)
+            nc.vector.tensor_tensor(
+                out=st[:, 0, :, :],
+                in0=st[:, 0, :, :],
+                in1=beta64[:].unsqueeze(2).to_broadcast([P, 4, GB]),
+                op=ALU.add,
+            )
+            stj = small.tile([P, 2, GB], F32, tag="stj", name="stj")
+            nc.vector.tensor_reduce(
+                out=stj[:], in_=st[:].rearrange("p a j b -> p a b j"), axis=AX.X, op=ALU.add
+            )
+            mvp = psum.tile([P, 2, GB], F32, tag="mv", name="mvp")
+            nc.tensor.matmul(
+                out=mvp[:].rearrange("p a b -> p (a b)"),
+                lhsT=bd[:].rearrange("p g d -> p (g d)"),
+                rhs=stj[:].rearrange("p a b -> p (a b)"),
+                start=True,
+                stop=True,
+            )
+            mv = small.tile([P, 2, GB], F32, tag="mvs", name="mv")
+            nc.vector.tensor_copy(out=mv[:], in_=mvp[:])
+            msq = small.tile([P, GB], F32, tag="msq", name="msq")
+            nc.vector.tensor_mul(out=msq[:], in0=mv[:, 0, :], in1=mv[:, 0, :])
+            var = small.tile([P, GB], F32, tag="var", name="var")
+            nc.vector.scalar_tensor_tensor(
+                out=var[:], in0=mv[:, 1, :], scalar=EPS, in1=msq[:], op0=ALU.add, op1=ALU.subtract
+            )
+            std = small.tile([P, GB], F32, tag="std", name="std")
+            nc.scalar.activation(out=std[:], in_=var[:], func=ACT.Sqrt)
+            rstd = small.tile([P, GB], F32, tag="rstd", name="rstd")
+            nc.vector.reciprocal(out=rstd[:], in_=std[:])
+            sc = small.tile([P, 4, GB], F32, tag="sc", name="sc")
+            nc.vector.tensor_tensor(
+                out=sc[:],
+                in0=gam[:].unsqueeze(2).to_broadcast([P, 4, GB]),
+                in1=rstd[:].unsqueeze(1).to_broadcast([P, 4, GB]),
+                op=ALU.mult,
+            )
+            d1 = small.tile([P, 4, GB], F32, tag="d1", name="d1")
+            nc.vector.tensor_tensor(
+                out=d1[:],
+                in0=beta[:].unsqueeze(2).to_broadcast([P, 4, GB]),
+                in1=mv[:, 0, :].unsqueeze(1).to_broadcast([P, 4, GB]),
+                op=ALU.subtract,
+            )
+            d2 = small.tile([P, 4, GB], F32, tag="d2", name="d2")
+            nc.vector.tensor_mul(out=d2[:], in0=d1[:], in1=sc[:])
+            sh = small.tile([P, 4, GB], F32, tag="sh", name="sh")
+            nc.vector.tensor_tensor(
+                out=sh[:],
+                in0=d2[:],
+                in1=bet2[:].unsqueeze(2).to_broadcast([P, 4, GB]),
+                op=ALU.add,
+            )
+            for j in range(4):
+                for bi in range(GB):
+                    nc.scalar.activation(
+                        out=res[:, g * GB + bi, j, :],
+                        in_=ys[j][:, bi, :],
+                        func=ACT.Relu,
+                        bias=sh[:, j, bi:bi + 1],
+                        scale=sc[:, j, bi:bi + 1],
+                    )
+
+        for i in range(NB + 4):
+            if 1 <= i + 1 < NB:
+                load(i + 1)
+            if i < NB:
+                tables(i)
+            if 0 <= i - 1 < NB:
+                flip_store(i - 1)
+            if 0 <= i - 2 < NB:
+                gather(i - 2)
+            if 0 <= i - 3 < NB:
+                finish(i - 3)
+                if (i - 3) % GB == GB - 1:
+                    conv_norm((i - 3) // GB)
+
+        for g in range(NB // GB):
+            nc.sync.dma_start(
+                out=out_final[:, g * GB:(g + 1) * GB, :],
+                in_=res[:, g * GB:(g + 1) * GB, :, :].rearrange("p b j n -> p b (j n)"),
+            )

@@ -21,9 +21,11 @@ NN = 64
 LEVELS = 8
 GB = 8
 SLOTS = 3
-SLOT_ROWS = 4096
+CHUNKS = 15
+SLOT_ROWS = 2 * CHUNKS * 128
 SLOT_WORDS = SLOT_ROWS * P
 EPS = 1e-5
+TPB = 6
 
 FLOPS = 2 * 48 * 512 * 512 * 64
 
@@ -33,6 +35,8 @@ def level_cols(k):
         return NT
     if k == 1:
         return NT - 1
+    if k == LEVELS - 1:
+        return P
     return NT + 2 - 2 ** k
 
 
@@ -88,7 +92,7 @@ def tile_coarsepyramid_pb_kernel(
         nc.sync.dma_start(out=pb_e[:], in_=be_roi.rearrange("(m j) -> m j", j=4))
 
         for i in range(SLOTS):
-            for k in range(1, LEVELS):
+            for k in range(1, LEVELS - 1):
                 nc.vector.memset(tabs[i][:, :, k, :, level_cols(k):NT], 0.0)
 
         W2 = 2 * NN
@@ -143,18 +147,26 @@ def tile_coarsepyramid_pb_kernel(
         nc.vector.tensor_copy(out=st_f[:], in_=st_i[:])
 
         idx_f = []
-        for a, (t_ap, zbase) in enumerate(((lo, 94), (tbb[:], 2078))):
+        k7 = keep.tile([P, W2], F32, name="k7")
+        nc.vector.tensor_scalar(
+            out=k7[:], in0=kk[:], scalar1=float(LEVELS - 1), scalar2=3806.0, op0=ALU.is_ge, op1=ALU.mult
+        )
+        g7 = keep.tile([P, W2], F32, name="g7")
+        nc.vector.tensor_scalar_add(out=g7[:], in0=k7[:], scalar1=-3838.0)
+        for a, (t_ap, zbase) in enumerate(((lo, 2006), (tbb[:], 2876))):
             z_i = keep.tile([P, W2], I32, name="z_i%d" % a)
-            nc.gpsimd.iota(z_i[:], pattern=[[32, NN], [1, 2]], base=zbase, channel_multiplier=0)
+            nc.gpsimd.iota(
+                z_i[:], pattern=[[0, 2], [30, 32], [1, 2]], base=zbase, channel_multiplier=0
+            )
             z_f = keep.tile([P, W2], F32, name="z_f%d" % a)
             nc.vector.tensor_copy(out=z_f[:], in_=z_i[:])
+            g0 = keep.tile([P, W2], F32, name="g0_%d" % a)
+            nc.vector.tensor_single_scalar(out=g0[:], in_=t_ap, scalar=128.0, op=ALU.is_ge)
             g1 = keep.tile([P, W2], F32, name="g1_%d" % a)
-            nc.vector.tensor_scalar(
-                out=g1[:], in0=t_ap, scalar1=128.0, scalar2=-4094.0, op0=ALU.is_ge, op1=ALU.mult
-            )
+            nc.vector.tensor_mul(out=g1[:], in0=g0[:], in1=g7[:])
             r1 = keep.tile([P, W2], F32, name="r1_%d" % a)
             nc.vector.scalar_tensor_tensor(
-                out=r1[:], in0=t_ap, scalar=32.0, in1=g1[:], op0=ALU.mult, op1=ALU.add
+                out=r1[:], in0=t_ap, scalar=30.0, in1=g1[:], op0=ALU.mult, op1=ALU.add
             )
             r2 = keep.tile([P, W2], F32, name="r2_%d" % a)
             nc.vector.scalar_tensor_tensor(
@@ -170,7 +182,7 @@ def tile_coarsepyramid_pb_kernel(
             nc.vector.tensor_add(out=r6[:], in0=r5[:], in1=z_f[:])
             idx_f.append(r6)
 
-        pidx = psum.tile([P, 2, P], F32, tag="tp", bufs=2, name="pidx")
+        pidx = psum.tile([P, 2, P], F32, tag="tp", bufs=TPB, name="pidx")
         for a in range(2):
             nc.tensor.transpose(pidx[:, a, :], idx_f[a][:], ident_f[:])
         idx_i = keep.tile([P, 2, NB], I32, name="idx_i")
@@ -191,7 +203,7 @@ def tile_coarsepyramid_pb_kernel(
             .rearrange("p (j m u) -> p j m u", j=4, u=2)
         )
         for jj in range(2):
-            pw = psum.tile([P, 2, 2, P], F32, tag="tp", bufs=2, name="pw")
+            pw = psum.tile([P, 2, 2, P], F32, tag="tp", bufs=TPB, name="pw")
             for jl in range(2):
                 w_words = w_sb[:, 2 * jj + jl, :].bitcast(F32)
                 for u in range(2):
@@ -240,25 +252,43 @@ def tile_coarsepyramid_pb_kernel(
                     in1=t[:, :, k - 1, :, sh:sh + n],
                     op=ALU.max,
                 )
+                if k == LEVELS - 2:
+                    nc.vector.tensor_tensor(
+                        out=t[:, :, k, :, NT - 1:NT],
+                        in0=t[:, :, k, :, P:P + 1],
+                        in1=t[:, :, k, :, P + 64:P + 65],
+                        op=ALU.max,
+                    )
 
-        def flip_store(b):
+        staged = {}
+
+        def flip(b):
             t = tabs[b % SLOTS]
-            stg = stage.tile([P, LEVELS, 2, 2, 2, P], BF16, tag="stg", name="stg")
+            stg = stage.tile([P, CHUNKS * 4 * P], BF16, tag="stg", name="stg")
+            stg_f = stg[:].bitcast(F32)
             for k in range(LEVELS):
-                pt = psum.tile([P, 2, 2, 2, P], BF16, tag="tp", bufs=2, name="pt")
-                for h in range(2):
+                halves = 2 if k < LEVELS - 1 else 1
+                pt = psum.tile([P, 8 * P], BF16, tag="tp", bufs=TPB, name="pt")
+                for h in range(halves):
                     for s in range(2):
                         for e in range(2):
+                            c0 = ((h * 2 + s) * 2 + e) * P
                             nc.tensor.transpose(
-                                pt[:, h, s, e, :], t[:, s, k, e, P * h:P * h + P], ident_b[:]
+                                pt[:, c0:c0 + P], t[:, s, k, e, P * h:P * h + P], ident_b[:]
                             )
-                nc.scalar.copy(out=stg[:, k, :, :, :, :], in_=pt[:])
+                nw = halves * 2 * P
+                nc.scalar.copy(
+                    out=stg_f[:, 4 * P * k:4 * P * k + nw], in_=pt[:].bitcast(F32)[:, 0:nw]
+                )
+            staged[b] = stg_f
+
+        def store(b):
             slot = b % SLOTS
-            nc.scalar.dma_start(
+            nc.sync.dma_start(
                 out=out_flat[slot * SLOT_WORDS:(slot + 1) * SLOT_WORDS].rearrange(
                     "(p w) -> p w", p=P
                 ),
-                in_=stg[:].rearrange("p k h s e c -> p (k h s e c)").bitcast(F32),
+                in_=staged[b],
             )
 
         gathered = {}
@@ -306,7 +336,7 @@ def tile_coarsepyramid_pb_kernel(
             )
             ys = []
             for j in range(4):
-                y = psum.tile([P, GB, NN], F32, tag="y%d" % j, name="y%d" % j)
+                y = psum.tile([P, GB, NN], F32, tag="tp", bufs=TPB, name="y%d" % j)
                 nc.tensor.matmul_mx(
                     out=y[:].rearrange("p b n -> p (b n)"),
                     lhsT=wq[:, P * j:P * j + P].bitcast(FP8X4),
@@ -394,9 +424,11 @@ def tile_coarsepyramid_pb_kernel(
             if i < NB:
                 tables(i)
             if 0 <= i - 1 < NB:
-                flip_store(i - 1)
+                flip(i - 1)
             if 0 <= i - 2 < NB:
                 gather(i - 2)
+            if 0 <= i - 1 < NB:
+                store(i - 1)
             if 0 <= i - 3 < NB:
                 finish(i - 3)
                 if (i - 3) % GB == GB - 1:

@@ -18,26 +18,23 @@ P = 128
 NB = 48
 NT = 256
 NN = 64
-LEVELS = 8
 GB = 8
-SLOTS = 3
-CHUNKS = 15
-SLOT_ROWS = 2 * CHUNKS * 128
+LOOKUPS = 3
+THRESH = (4.0, 12.0, 36.0, 108.0)
+SIZE_STEP = (3.0, 8.0, 24.0, 72.0)
+ROW_STEP = (256.0, 254.0, 246.0, 222.0)
+O1, O2, O3, O4, OZ = 0, 254, 500, 722, 872
+UPPER = 896
+ZERO_ROW = NT + OZ
+CHUNKS = 9
+SLOTS = 5
+SLOT_ROWS = 2 * CHUNKS * P
 SLOT_WORDS = SLOT_ROWS * P
-EPS = 1e-5
+NTAB = 3
 TPB = 6
+EPS = 1e-5
 
 FLOPS = 2 * 48 * 512 * 512 * 64
-
-
-def level_cols(k):
-    if k == 0:
-        return NT
-    if k == 1:
-        return NT - 1
-    if k == LEVELS - 1:
-        return P
-    return NT + 2 - 2 ** k
 
 
 def tile_coarsepyramid_pb_kernel(
@@ -46,8 +43,9 @@ def tile_coarsepyramid_pb_kernel(
     nc = tc.nc
     with ExitStack() as ctx:
         keep = ctx.enter_context(tc.tile_pool(name="keep", bufs=1))
-        stage = ctx.enter_context(tc.tile_pool(name="stage", bufs=3))
-        gat = ctx.enter_context(tc.tile_pool(name="gat", bufs=4))
+        xin = ctx.enter_context(tc.tile_pool(name="xin", bufs=6))
+        stage = ctx.enter_context(tc.tile_pool(name="stage", bufs=5))
+        gat = ctx.enter_context(tc.tile_pool(name="gat", bufs=6))
         grpp = ctx.enter_context(tc.tile_pool(name="grpp", bufs=2))
         small = ctx.enter_context(tc.tile_pool(name="small", bufs=2))
         psum = ctx.enter_context(tc.psum_pool(name="psum", bufs=1))
@@ -70,17 +68,17 @@ def tile_coarsepyramid_pb_kernel(
         nc.vector.memset(segb[:], 0.0)
         nc.sync.dma_start(out=segb[0:NB, :], in_=frame_segments.rearrange("b n f -> b (n f)"))
 
-        tabs = []
-        for i in range(SLOTS):
-            tabs.append(keep.tile([P, 2, LEVELS, 2, NT], BF16, name="tab%d" % i))
+        frames = {}
 
         def load(b):
+            x0 = xin.tile([P, 2, 2, NT], BF16, tag="x0", name="x0")
             nc.sync.dma_start(
-                out=tabs[b % SLOTS][:, :, 0, :, :],
-                in_=frame_level_feature[b].rearrange("(s p e) t -> p s e t", s=2, e=2),
+                out=x0[:], in_=frame_level_feature[b].rearrange("(s p e) t -> p s e t", s=2, e=2)
             )
+            frames[b] = x0
 
         load(0)
+        load(1)
 
         w_sb = keep.tile([P, 4, 512], BF16, name="w_sb")
         nc.sync.dma_start(out=w_sb[:], in_=w_roi.rearrange("(m j) c -> m j c", j=4))
@@ -90,10 +88,19 @@ def tile_coarsepyramid_pb_kernel(
         nc.sync.dma_start(out=pb_g[:], in_=g_roi.rearrange("(m j) -> m j", j=4))
         pb_e = keep.tile([P, 4], BF16, name="pb_e")
         nc.sync.dma_start(out=pb_e[:], in_=be_roi.rearrange("(m j) -> m j", j=4))
+        load(2)
 
-        for i in range(SLOTS):
-            for k in range(1, LEVELS - 1):
-                nc.vector.memset(tabs[i][:, :, k, :, level_cols(k):NT], 0.0)
+        uppers = []
+        shifted = []
+        for i in range(NTAB):
+            up = keep.tile([P, 2, 2, UPPER], BF16, name="up%d" % i)
+            nc.vector.memset(up[:, :, :, OZ:UPPER], 0.0)
+            uppers.append(up)
+            x1 = keep.tile([P, 2, 2, NT], BF16, name="x1_%d" % i)
+            nc.vector.memset(x1[:], 0.0)
+            shifted.append(x1)
+        tmp_a = keep.tile([P, 2, 2, NT], BF16, name="tmp_a")
+        tmp_b = keep.tile([P, 2, 2, NT], BF16, name="tmp_b")
 
         W2 = 2 * NN
         sf = keep.tile([P, 2 * W2], F32, name="sf")
@@ -120,72 +127,82 @@ def tile_coarsepyramid_pb_kernel(
         nc.vector.tensor_scalar(
             out=lc[:], in0=ld[:], scalar1=0.0, scalar2=1.0, op0=ALU.max, op1=ALU.add
         )
-        s2i = keep.tile([P, W2], I32, name="s2i")
-        nc.vector.tensor_single_scalar(
-            out=s2i[:], in_=lc[:].bitcast(I32), scalar=0x7F800000, op=ALU.bitwise_and
-        )
-        kei = keep.tile([P, W2], I32, name="kei")
-        nc.vector.tensor_single_scalar(
-            out=kei[:], in_=lc[:].bitcast(I32), scalar=23, op=ALU.logical_shift_right
-        )
-        kf = keep.tile([P, W2], F32, name="kf")
-        nc.vector.tensor_copy(out=kf[:], in_=kei[:])
-        kk = keep.tile([P, W2], F32, name="kk")
-        nc.vector.tensor_scalar(
-            out=kk[:], in0=kf[:], scalar1=-127.0, scalar2=float(LEVELS - 1), op0=ALU.add, op1=ALU.min
-        )
-        s2 = keep.tile([P, W2], F32, name="s2")
-        nc.vector.tensor_scalar_min(out=s2[:], in0=s2i[:].bitcast(F32), scalar1=128.0)
-        tb0 = keep.tile([P, W2], F32, name="tb0")
-        nc.vector.tensor_sub(out=tb0[:], in0=hi, in1=s2[:])
-        tbb = keep.tile([P, W2], F32, name="tbb")
-        nc.vector.tensor_scalar_add(out=tbb[:], in0=tb0[:], scalar1=1.0)
+        size = keep.tile([P, W2], F32, name="size")
+        nc.vector.memset(size[:], 1.0)
+        roff = keep.tile([P, W2], F32, name="roff")
+        nc.vector.memset(roff[:], 0.0)
+        for j in range(4):
+            cj = keep.tile([P, W2], F32, name="cj%d" % j)
+            nc.vector.tensor_single_scalar(out=cj[:], in_=lc[:], scalar=THRESH[j], op=ALU.is_ge)
+            nc.vector.scalar_tensor_tensor(
+                out=size[:], in0=cj[:], scalar=SIZE_STEP[j], in1=size[:], op0=ALU.mult, op1=ALU.add
+            )
+            nc.vector.scalar_tensor_tensor(
+                out=roff[:], in0=cj[:], scalar=ROW_STEP[j], in1=roff[:], op0=ALU.mult, op1=ALU.add
+            )
+        t_last0 = keep.tile([P, W2], F32, name="t_last0")
+        nc.vector.tensor_sub(out=t_last0[:], in0=hi, in1=size[:])
+        t_last = keep.tile([P, W2], F32, name="t_last")
+        nc.vector.tensor_scalar_add(out=t_last[:], in0=t_last0[:], scalar1=1.0)
+        t_mid0 = keep.tile([P, W2], F32, name="t_mid0")
+        nc.vector.tensor_add(out=t_mid0[:], in0=lo, in1=size[:])
+        t_mid = keep.tile([P, W2], F32, name="t_mid")
+        nc.vector.tensor_tensor(out=t_mid[:], in0=t_mid0[:], in1=t_last[:], op=ALU.min)
 
+        zr_i = keep.tile([P, W2], I32, name="zr_i")
+        nc.gpsimd.iota(
+            zr_i[:], pattern=[[0, 4], [1, 16], [0, 2]], base=ZERO_ROW, channel_multiplier=0
+        )
+        zr = keep.tile([P, W2], F32, name="zr")
+        nc.vector.tensor_copy(out=zr[:], in_=zr_i[:])
         st_i = keep.tile([P, W2], I32, name="st_i")
         nc.gpsimd.iota(st_i[:], pattern=[[0, NN], [1, 2]], base=0, channel_multiplier=0)
         st_f = keep.tile([P, W2], F32, name="st_f")
         nc.vector.tensor_copy(out=st_f[:], in_=st_i[:])
 
-        idx_f = []
-        k7 = keep.tile([P, W2], F32, name="k7")
-        nc.vector.tensor_scalar(
-            out=k7[:], in0=kk[:], scalar1=float(LEVELS - 1), scalar2=3806.0, op0=ALU.is_ge, op1=ALU.mult
-        )
-        g7 = keep.tile([P, W2], F32, name="g7")
-        nc.vector.tensor_scalar_add(out=g7[:], in0=k7[:], scalar1=-3838.0)
-        for a, (t_ap, zbase) in enumerate(((lo, 2006), (tbb[:], 2876))):
-            z_i = keep.tile([P, W2], I32, name="z_i%d" % a)
-            nc.gpsimd.iota(
-                z_i[:], pattern=[[0, 2], [30, 32], [1, 2]], base=zbase, channel_multiplier=0
-            )
-            z_f = keep.tile([P, W2], F32, name="z_f%d" % a)
-            nc.vector.tensor_copy(out=z_f[:], in_=z_i[:])
-            g0 = keep.tile([P, W2], F32, name="g0_%d" % a)
-            nc.vector.tensor_single_scalar(out=g0[:], in_=t_ap, scalar=128.0, op=ALU.is_ge)
-            g1 = keep.tile([P, W2], F32, name="g1_%d" % a)
-            nc.vector.tensor_mul(out=g1[:], in0=g0[:], in1=g7[:])
-            r1 = keep.tile([P, W2], F32, name="r1_%d" % a)
-            nc.vector.scalar_tensor_tensor(
-                out=r1[:], in0=t_ap, scalar=30.0, in1=g1[:], op0=ALU.mult, op1=ALU.add
-            )
-            r2 = keep.tile([P, W2], F32, name="r2_%d" % a)
-            nc.vector.scalar_tensor_tensor(
-                out=r2[:], in0=kk[:], scalar=4.0, in1=r1[:], op0=ALU.mult, op1=ALU.add
-            )
-            r3 = keep.tile([P, W2], F32, name="r3_%d" % a)
-            nc.vector.tensor_add(out=r3[:], in0=r2[:], in1=st_f[:])
-            r4 = keep.tile([P, W2], F32, name="r4_%d" % a)
-            nc.vector.tensor_sub(out=r4[:], in0=r3[:], in1=z_f[:])
-            r5 = keep.tile([P, W2], F32, name="r5_%d" % a)
-            nc.vector.tensor_mul(out=r5[:], in0=r4[:], in1=ne[:])
-            r6 = keep.tile([P, W2], F32, name="r6_%d" % a)
-            nc.vector.tensor_add(out=r6[:], in0=r5[:], in1=z_f[:])
-            idx_f.append(r6)
+        rr = keep.tile([P, LOOKUPS, W2], F32, name="rr")
+        for a, t_ap in enumerate((lo, t_mid[:], t_last[:])):
+            nc.vector.tensor_add(out=rr[:, a, :], in0=roff[:], in1=t_ap)
 
-        pidx = psum.tile([P, 2, P], F32, tag="tp", bufs=TPB, name="pidx")
-        for a in range(2):
-            nc.tensor.transpose(pidx[:, a, :], idx_f[a][:], ident_f[:])
-        idx_i = keep.tile([P, 2, NB], I32, name="idx_i")
+        def over_lookups(ap):
+            return ap.unsqueeze(1).to_broadcast([P, LOOKUPS, W2])
+
+        r1 = keep.tile([P, LOOKUPS, W2], F32, name="r1")
+        nc.vector.tensor_tensor(out=r1[:], in0=rr[:], in1=over_lookups(zr[:]), op=ALU.subtract)
+        r2 = keep.tile([P, LOOKUPS, W2], F32, name="r2")
+        nc.vector.tensor_tensor(out=r2[:], in0=r1[:], in1=over_lookups(ne[:]), op=ALU.mult)
+        r3 = keep.tile([P, LOOKUPS, W2], F32, name="r3")
+        nc.vector.tensor_tensor(out=r3[:], in0=r2[:], in1=over_lookups(zr[:]), op=ALU.add)
+        ri = keep.tile([P, LOOKUPS, W2], I32, name="ri")
+        nc.vector.tensor_copy(out=ri[:], in_=r3[:])
+        rlo_i = keep.tile([P, LOOKUPS, W2], I32, name="rlo_i")
+        nc.vector.tensor_single_scalar(out=rlo_i[:], in_=ri[:], scalar=P - 1, op=ALU.bitwise_and)
+        rhi_i = keep.tile([P, LOOKUPS, W2], I32, name="rhi_i")
+        nc.vector.tensor_single_scalar(
+            out=rhi_i[:], in_=ri[:], scalar=7, op=ALU.logical_shift_right
+        )
+        rlo = keep.tile([P, LOOKUPS, W2], F32, name="rlo")
+        nc.vector.tensor_copy(out=rlo[:], in_=rlo_i[:])
+        rhi = keep.tile([P, LOOKUPS, W2], F32, name="rhi")
+        nc.vector.tensor_copy(out=rhi[:], in_=rhi_i[:])
+        x2 = keep.tile([P, LOOKUPS, W2], F32, name="x2")
+        nc.vector.scalar_tensor_tensor(
+            out=x2[:].rearrange("p a w -> p (a w)"),
+            in0=rlo[:].rearrange("p a w -> p (a w)"),
+            scalar=float(2 * CHUNKS),
+            in1=rhi[:].rearrange("p a w -> p (a w)"),
+            op0=ALU.mult,
+            op1=ALU.add,
+        )
+        x3 = keep.tile([P, LOOKUPS, W2], F32, name="x3")
+        nc.vector.tensor_add(out=x3[:], in0=x2[:], in1=rhi[:])
+        x4 = keep.tile([P, LOOKUPS, W2], F32, name="x4")
+        nc.vector.tensor_tensor(out=x4[:], in0=x3[:], in1=over_lookups(st_f[:]), op=ALU.add)
+
+        pidx = psum.tile([P, LOOKUPS, P], F32, tag="tp", bufs=TPB, name="pidx")
+        for a in range(LOOKUPS):
+            nc.tensor.transpose(pidx[:, a, :], x4[:, a, :], ident_f[:])
+        idx_i = keep.tile([P, LOOKUPS, NB], I32, name="idx_i")
         for j in range(SLOTS):
             nc.vector.tensor_scalar(
                 out=idx_i[:, :, j:NB:SLOTS],
@@ -241,61 +258,68 @@ def tile_coarsepyramid_pb_kernel(
 
         res = keep.tile([P, NB, 4, NN], F32, name="res")
 
+        def shift(b):
+            nc.scalar.copy(
+                out=shifted[b % NTAB][:, :, :, 0:NT - 1], in_=frames[b][:, :, :, 1:NT]
+            )
+
+        def vmax(dst, d0, src0, a0, src1, b0, n):
+            nc.vector.tensor_tensor(
+                out=dst[:, :, :, d0:d0 + n],
+                in0=src0[:, :, :, a0:a0 + n],
+                in1=src1[:, :, :, b0:b0 + n],
+                op=ALU.max,
+            )
+
         def tables(b):
-            t = tabs[b % SLOTS]
-            for k in range(1, LEVELS):
-                sh = 2 ** (k - 1)
-                n = level_cols(k)
-                nc.vector.tensor_tensor(
-                    out=t[:, :, k, :, 0:n],
-                    in0=t[:, :, k - 1, :, 0:n],
-                    in1=t[:, :, k - 1, :, sh:sh + n],
-                    op=ALU.max,
-                )
-                if k == LEVELS - 2:
-                    nc.vector.tensor_tensor(
-                        out=t[:, :, k, :, NT - 1:NT],
-                        in0=t[:, :, k, :, P:P + 1],
-                        in1=t[:, :, k, :, P + 64:P + 65],
-                        op=ALU.max,
-                    )
+            x0 = frames[b]
+            up = uppers[b % NTAB]
+            vmax(tmp_a, 0, x0, 0, shifted[b % NTAB], 0, 256)
+            vmax(up, O1, tmp_a, 0, tmp_a, 2, 254)
+            vmax(tmp_b, 0, up, O1, up, O1 + 4, 250)
+            vmax(up, O2, tmp_b, 0, up, O1 + 8, 246)
+            vmax(tmp_a, 0, up, O2, up, O2 + 12, 234)
+            vmax(up, O3, tmp_a, 0, up, O2 + 24, 222)
+            vmax(tmp_b, 0, up, O3, up, O3 + 36, 186)
+            vmax(up, O4, tmp_b, 0, up, O3 + 72, 150)
 
         staged = {}
 
         def flip(b):
-            t = tabs[b % SLOTS]
+            x0 = frames[b]
+            up = uppers[b % NTAB]
             stg = stage.tile([P, CHUNKS * 4 * P], BF16, tag="stg", name="stg")
             stg_f = stg[:].bitcast(F32)
-            for k in range(LEVELS):
-                halves = 2 if k < LEVELS - 1 else 1
+            for q0 in range(0, CHUNKS, 2):
+                nq = min(2, CHUNKS - q0)
                 pt = psum.tile([P, 8 * P], BF16, tag="tp", bufs=TPB, name="pt")
-                for h in range(halves):
+                for qi in range(nq):
+                    q = q0 + qi
                     for s in range(2):
                         for e in range(2):
-                            c0 = ((h * 2 + s) * 2 + e) * P
-                            nc.tensor.transpose(
-                                pt[:, c0:c0 + P], t[:, s, k, e, P * h:P * h + P], ident_b[:]
-                            )
-                nw = halves * 2 * P
+                            c0 = ((qi * 2 + s) * 2 + e) * P
+                            if q < 2:
+                                src = x0[:, s, e, P * q:P * q + P]
+                            else:
+                                src = up[:, s, e, P * (q - 2):P * (q - 2) + P]
+                            nc.tensor.transpose(pt[:, c0:c0 + P], src, ident_b[:])
                 nc.scalar.copy(
-                    out=stg_f[:, 4 * P * k:4 * P * k + nw], in_=pt[:].bitcast(F32)[:, 0:nw]
+                    out=stg_f[:, 2 * P * q0:2 * P * (q0 + nq)],
+                    in_=pt[:].bitcast(F32)[:, 0:2 * P * nq],
                 )
             staged[b] = stg_f
 
         def store(b):
-            slot = b % SLOTS
+            w0 = (b % SLOTS) * SLOT_WORDS
             nc.sync.dma_start(
-                out=out_flat[slot * SLOT_WORDS:(slot + 1) * SLOT_WORDS].rearrange(
-                    "(p w) -> p w", p=P
-                ),
-                in_=staged[b],
+                out=out_flat[w0:w0 + SLOT_WORDS].rearrange("(p w) -> p w", p=P), in_=staged[b]
             )
 
         gathered = {}
 
         def gather(b):
-            pair = []
-            for a in range(2):
+            got = []
+            for a in range(LOOKUPS):
                 g = gat.tile([P, 2 * P], BF16, tag="g%d" % a, name="g%d" % a)
                 nc.gpsimd.indirect_dma_start(
                     out=g[:].bitcast(F32),
@@ -303,15 +327,17 @@ def tile_coarsepyramid_pb_kernel(
                     in_=out_rows[0:(b % SLOTS + 1) * SLOT_ROWS, :],
                     in_offset=bass.IndirectOffsetOnAxis(ap=idx_i[:, a, b:b + 1], axis=0),
                 )
-                pair.append(g)
-            gathered[b] = pair
+                got.append(g)
+            gathered[b] = got
 
         groups = {}
 
         def finish(b):
-            ga, gb = gathered[b]
+            g0, g1, g2 = gathered[b]
+            pm0 = gat.tile([P, 2 * P], BF16, tag="pm0", name="pm0")
+            nc.vector.tensor_tensor(out=pm0[:], in0=g0[:], in1=g1[:], op=ALU.max)
             pm = gat.tile([P, 2 * P], BF16, tag="pm", name="pm")
-            nc.vector.tensor_tensor(out=pm[:], in0=ga[:], in1=gb[:], op=ALU.max)
+            nc.vector.tensor_tensor(out=pm[:], in0=pm0[:], in1=g2[:], op=ALU.max)
             pp = psum.tile([P, 2, P], BF16, tag="pp", name="pp")
             for e in range(2):
                 nc.tensor.transpose(pp[:, e, :], pm[:, P * e:P * e + P], ident_b[:])
@@ -418,9 +444,12 @@ def tile_coarsepyramid_pb_kernel(
                         scale=sc[:, j, bi:bi + 1],
                     )
 
+        shift(0)
         for i in range(NB + 4):
+            if 3 <= i + 3 < NB:
+                load(i + 3)
             if 1 <= i + 1 < NB:
-                load(i + 1)
+                shift(i + 1)
             if i < NB:
                 tables(i)
             if 0 <= i - 1 < NB:
@@ -429,10 +458,10 @@ def tile_coarsepyramid_pb_kernel(
                 gather(i - 2)
             if 0 <= i - 1 < NB:
                 store(i - 1)
-            if 0 <= i - 3 < NB:
-                finish(i - 3)
-                if (i - 3) % GB == GB - 1:
-                    conv_norm((i - 3) // GB)
+            if 0 <= i - 4 < NB:
+                finish(i - 4)
+                if (i - 4) % GB == GB - 1:
+                    conv_norm((i - 4) // GB)
 
         for g in range(NB // GB):
             nc.sync.dma_start(

@@ -18,7 +18,7 @@ P = 128
 NB = 48
 NT = 256
 NN = 64
-GB = 8
+W2 = 2 * NN
 LOOKUPS = 3
 THRESH = (4.0, 12.0, 36.0, 108.0)
 SIZE_STEP = (3.0, 8.0, 24.0, 72.0)
@@ -32,6 +32,7 @@ SLOT_ROWS = 2 * CHUNKS * P
 SLOT_WORDS = SLOT_ROWS * P
 NTAB = 3
 TPB = 6
+GROUPS = (8, 8, 8, 8, 8, 4, 2, 2)
 EPS = 1e-5
 
 FLOPS = 2 * 48 * 512 * 512 * 64
@@ -41,6 +42,13 @@ def tile_coarsepyramid_pb_kernel(
     tc, frame_level_feature, frame_segments, w_roi, b_roi, g_roi, be_roi, out
 ):
     nc = tc.nc
+    group_of = {}
+    b_first = 0
+    for gi, nb in enumerate(GROUPS):
+        for bi in range(nb):
+            group_of[b_first + bi] = (gi, bi, nb, b_first)
+        b_first += nb
+
     with ExitStack() as ctx:
         keep = ctx.enter_context(tc.tile_pool(name="keep", bufs=1))
         xin = ctx.enter_context(tc.tile_pool(name="xin", bufs=6))
@@ -54,20 +62,7 @@ def tile_coarsepyramid_pb_kernel(
         out_rows = out_flat.rearrange("(r w) -> r w", w=P)
         out_final = out.rearrange("b (m j) n -> m b (j n)", j=4)
 
-        one = keep.tile([P, 1], F32, name="one")
-        nc.vector.memset(one[:], 1.0)
-        one2 = keep.tile([P, 1], F32, name="one2")
-        nc.scalar.activation(out=one2[:], in_=one[:], func=ACT.Sqrt)
-
-        ident_f = keep.tile([P, P], F32, name="ident_f")
-        make_identity(nc, ident_f[:])
-        ident_b = keep.tile([P, P], BF16, name="ident_b")
-        make_identity(nc, ident_b[:])
-
-        segb = keep.tile([P, 4 * NN], BF16, name="segb")
-        nc.vector.memset(segb[:], 0.0)
-        nc.sync.dma_start(out=segb[0:NB, :], in_=frame_segments.rearrange("b n f -> b (n f)"))
-
+        made = {}
         frames = {}
 
         def load(b):
@@ -78,8 +73,11 @@ def tile_coarsepyramid_pb_kernel(
             frames[b] = x0
 
         load(0)
+        segb = keep.tile([P, 4 * NN], BF16, name="segb")
+        nc.vector.memset(segb[:], 0.0)
+        nc.sync.dma_start(out=segb[0:NB, :], in_=frame_segments.rearrange("b n f -> b (n f)"))
         load(1)
-
+        load(2)
         w_sb = keep.tile([P, 4, 512], BF16, name="w_sb")
         nc.sync.dma_start(out=w_sb[:], in_=w_roi.rearrange("(m j) c -> m j c", j=4))
         pb_b = keep.tile([P, 4], BF16, name="pb_b")
@@ -88,175 +86,185 @@ def tile_coarsepyramid_pb_kernel(
         nc.sync.dma_start(out=pb_g[:], in_=g_roi.rearrange("(m j) -> m j", j=4))
         pb_e = keep.tile([P, 4], BF16, name="pb_e")
         nc.sync.dma_start(out=pb_e[:], in_=be_roi.rearrange("(m j) -> m j", j=4))
-        load(2)
+
+        one = keep.tile([P, 1], F32, name="one")
+        nc.vector.memset(one[:], 1.0)
+        one2 = keep.tile([P, 1], F32, name="one2")
+        nc.scalar.activation(out=one2[:], in_=one[:], func=ACT.Sqrt)
+
+        ident_b = keep.tile([P, P], BF16, name="ident_b")
+        make_identity(nc, ident_b[:])
+        ident_f = keep.tile([P, P], F32, name="ident_f")
+        make_identity(nc, ident_f[:])
 
         uppers = []
         shifted = []
         for i in range(NTAB):
-            up = keep.tile([P, 2, 2, UPPER], BF16, name="up%d" % i)
-            nc.vector.memset(up[:, :, :, OZ:UPPER], 0.0)
-            uppers.append(up)
             x1 = keep.tile([P, 2, 2, NT], BF16, name="x1_%d" % i)
             nc.vector.memset(x1[:], 0.0)
             shifted.append(x1)
+            up = keep.tile([P, 2, 2, UPPER], BF16, name="up%d" % i)
+            nc.vector.memset(up[:, :, :, OZ:UPPER], 0.0)
+            uppers.append(up)
         tmp_a = keep.tile([P, 2, 2, NT], BF16, name="tmp_a")
         tmp_b = keep.tile([P, 2, 2, NT], BF16, name="tmp_b")
-
-        W2 = 2 * NN
-        sf = keep.tile([P, 2 * W2], F32, name="sf")
-        nc.vector.tensor_scalar(
-            out=sf[:], in0=segb[:], scalar1=0.0, scalar2=float(NT - 1), op0=ALU.max, op1=ALU.min
-        )
-        si = keep.tile([P, 2 * W2], I32, name="si")
-        nc.vector.tensor_copy(out=si[:], in_=sf[:])
-        fi = keep.tile([P, 2 * W2], F32, name="fi")
-        nc.vector.tensor_copy(out=fi[:], in_=si[:])
-        gt = keep.tile([P, 2 * W2], F32, name="gt")
-        nc.vector.tensor_tensor(out=gt[:], in0=fi[:], in1=sf[:], op=ALU.is_gt)
-        fl = keep.tile([P, 2 * W2], F32, name="fl")
-        nc.vector.tensor_sub(out=fl[:], in0=fi[:], in1=gt[:])
-        fl2 = fl[:].rearrange("p (w e) -> p w e", e=2)
-        lo = fl2[:, :, 0]
-        hi = fl2[:, :, 1]
-
-        ld = keep.tile([P, W2], F32, name="ld")
-        nc.vector.tensor_sub(out=ld[:], in0=hi, in1=lo)
-        ne = keep.tile([P, W2], F32, name="ne")
-        nc.vector.tensor_single_scalar(out=ne[:], in_=ld[:], scalar=0.0, op=ALU.is_ge)
-        lc = keep.tile([P, W2], F32, name="lc")
-        nc.vector.tensor_scalar(
-            out=lc[:], in0=ld[:], scalar1=0.0, scalar2=1.0, op0=ALU.max, op1=ALU.add
-        )
-        size = keep.tile([P, W2], F32, name="size")
-        nc.vector.memset(size[:], 1.0)
-        roff = keep.tile([P, W2], F32, name="roff")
-        nc.vector.memset(roff[:], 0.0)
-        for j in range(4):
-            cj = keep.tile([P, W2], F32, name="cj%d" % j)
-            nc.vector.tensor_single_scalar(out=cj[:], in_=lc[:], scalar=THRESH[j], op=ALU.is_ge)
-            nc.vector.scalar_tensor_tensor(
-                out=size[:], in0=cj[:], scalar=SIZE_STEP[j], in1=size[:], op0=ALU.mult, op1=ALU.add
-            )
-            nc.vector.scalar_tensor_tensor(
-                out=roff[:], in0=cj[:], scalar=ROW_STEP[j], in1=roff[:], op0=ALU.mult, op1=ALU.add
-            )
-        t_last0 = keep.tile([P, W2], F32, name="t_last0")
-        nc.vector.tensor_sub(out=t_last0[:], in0=hi, in1=size[:])
-        t_last = keep.tile([P, W2], F32, name="t_last")
-        nc.vector.tensor_scalar_add(out=t_last[:], in0=t_last0[:], scalar1=1.0)
-        t_mid0 = keep.tile([P, W2], F32, name="t_mid0")
-        nc.vector.tensor_add(out=t_mid0[:], in0=lo, in1=size[:])
-        t_mid = keep.tile([P, W2], F32, name="t_mid")
-        nc.vector.tensor_tensor(out=t_mid[:], in0=t_mid0[:], in1=t_last[:], op=ALU.min)
-
-        zr_i = keep.tile([P, W2], I32, name="zr_i")
-        nc.gpsimd.iota(
-            zr_i[:], pattern=[[0, 4], [1, 16], [0, 2]], base=ZERO_ROW, channel_multiplier=0
-        )
-        zr = keep.tile([P, W2], F32, name="zr")
-        nc.vector.tensor_copy(out=zr[:], in_=zr_i[:])
-        st_i = keep.tile([P, W2], I32, name="st_i")
-        nc.gpsimd.iota(st_i[:], pattern=[[0, NN], [1, 2]], base=0, channel_multiplier=0)
-        st_f = keep.tile([P, W2], F32, name="st_f")
-        nc.vector.tensor_copy(out=st_f[:], in_=st_i[:])
-
-        rr = keep.tile([P, LOOKUPS, W2], F32, name="rr")
-        for a, t_ap in enumerate((lo, t_mid[:], t_last[:])):
-            nc.vector.tensor_add(out=rr[:, a, :], in0=roff[:], in1=t_ap)
+        res = keep.tile([P, NB, 4, NN], F32, name="res")
 
         def over_lookups(ap):
             return ap.unsqueeze(1).to_broadcast([P, LOOKUPS, W2])
 
-        r1 = keep.tile([P, LOOKUPS, W2], F32, name="r1")
-        nc.vector.tensor_tensor(out=r1[:], in0=rr[:], in1=over_lookups(zr[:]), op=ALU.subtract)
-        r2 = keep.tile([P, LOOKUPS, W2], F32, name="r2")
-        nc.vector.tensor_tensor(out=r2[:], in0=r1[:], in1=over_lookups(ne[:]), op=ALU.mult)
-        r3 = keep.tile([P, LOOKUPS, W2], F32, name="r3")
-        nc.vector.tensor_tensor(out=r3[:], in0=r2[:], in1=over_lookups(zr[:]), op=ALU.add)
-        ri = keep.tile([P, LOOKUPS, W2], I32, name="ri")
-        nc.vector.tensor_copy(out=ri[:], in_=r3[:])
-        rlo_i = keep.tile([P, LOOKUPS, W2], I32, name="rlo_i")
-        nc.vector.tensor_single_scalar(out=rlo_i[:], in_=ri[:], scalar=P - 1, op=ALU.bitwise_and)
-        rhi_i = keep.tile([P, LOOKUPS, W2], I32, name="rhi_i")
-        nc.vector.tensor_single_scalar(
-            out=rhi_i[:], in_=ri[:], scalar=7, op=ALU.logical_shift_right
-        )
-        rlo = keep.tile([P, LOOKUPS, W2], F32, name="rlo")
-        nc.vector.tensor_copy(out=rlo[:], in_=rlo_i[:])
-        rhi = keep.tile([P, LOOKUPS, W2], F32, name="rhi")
-        nc.vector.tensor_copy(out=rhi[:], in_=rhi_i[:])
-        x2 = keep.tile([P, LOOKUPS, W2], F32, name="x2")
-        nc.vector.scalar_tensor_tensor(
-            out=x2[:].rearrange("p a w -> p (a w)"),
-            in0=rlo[:].rearrange("p a w -> p (a w)"),
-            scalar=float(2 * CHUNKS),
-            in1=rhi[:].rearrange("p a w -> p (a w)"),
-            op0=ALU.mult,
-            op1=ALU.add,
-        )
-        x3 = keep.tile([P, LOOKUPS, W2], F32, name="x3")
-        nc.vector.tensor_add(out=x3[:], in0=x2[:], in1=rhi[:])
-        x4 = keep.tile([P, LOOKUPS, W2], F32, name="x4")
-        nc.vector.tensor_tensor(out=x4[:], in0=x3[:], in1=over_lookups(st_f[:]), op=ALU.add)
-
-        pidx = psum.tile([P, LOOKUPS, P], F32, tag="tp", bufs=TPB, name="pidx")
-        for a in range(LOOKUPS):
-            nc.tensor.transpose(pidx[:, a, :], x4[:, a, :], ident_f[:])
-        idx_i = keep.tile([P, LOOKUPS, NB], I32, name="idx_i")
-        for j in range(SLOTS):
+        def prep_rows():
+            sf = keep.tile([P, 2 * W2], F32, name="sf")
             nc.vector.tensor_scalar(
-                out=idx_i[:, :, j:NB:SLOTS],
-                in0=pidx[:, :, j:NB:SLOTS],
-                scalar1=float(SLOT_ROWS * j),
+                out=sf[:], in0=segb[:], scalar1=0.0, scalar2=float(NT - 1), op0=ALU.max, op1=ALU.min
+            )
+            si = keep.tile([P, 2 * W2], I32, name="si")
+            nc.vector.tensor_copy(out=si[:], in_=sf[:])
+            fi = keep.tile([P, 2 * W2], F32, name="fi")
+            nc.vector.tensor_copy(out=fi[:], in_=si[:])
+            gt = keep.tile([P, 2 * W2], F32, name="gt")
+            nc.vector.tensor_tensor(out=gt[:], in0=fi[:], in1=sf[:], op=ALU.is_gt)
+            fl = keep.tile([P, 2 * W2], F32, name="fl")
+            nc.vector.tensor_sub(out=fl[:], in0=fi[:], in1=gt[:])
+            fl2 = fl[:].rearrange("p (w e) -> p w e", e=2)
+            lo = fl2[:, :, 0]
+            hi = fl2[:, :, 1]
+
+            ld = keep.tile([P, W2], F32, name="ld")
+            nc.vector.tensor_sub(out=ld[:], in0=hi, in1=lo)
+            ne = keep.tile([P, W2], F32, name="ne")
+            nc.vector.tensor_single_scalar(out=ne[:], in_=ld[:], scalar=0.0, op=ALU.is_ge)
+            lc = keep.tile([P, W2], F32, name="lc")
+            nc.vector.tensor_scalar(
+                out=lc[:], in0=ld[:], scalar1=0.0, scalar2=1.0, op0=ALU.max, op1=ALU.add
+            )
+            size = keep.tile([P, W2], F32, name="size")
+            nc.vector.memset(size[:], 1.0)
+            roff = keep.tile([P, W2], F32, name="roff")
+            nc.vector.memset(roff[:], 0.0)
+            for j in range(4):
+                cj = keep.tile([P, W2], F32, name="cj%d" % j)
+                nc.vector.tensor_single_scalar(out=cj[:], in_=lc[:], scalar=THRESH[j], op=ALU.is_ge)
+                nc.vector.scalar_tensor_tensor(
+                    out=size[:], in0=cj[:], scalar=SIZE_STEP[j], in1=size[:], op0=ALU.mult, op1=ALU.add
+                )
+                nc.vector.scalar_tensor_tensor(
+                    out=roff[:], in0=cj[:], scalar=ROW_STEP[j], in1=roff[:], op0=ALU.mult, op1=ALU.add
+                )
+            t_last0 = keep.tile([P, W2], F32, name="t_last0")
+            nc.vector.tensor_sub(out=t_last0[:], in0=hi, in1=size[:])
+            t_last = keep.tile([P, W2], F32, name="t_last")
+            nc.vector.tensor_scalar_add(out=t_last[:], in0=t_last0[:], scalar1=1.0)
+            t_mid0 = keep.tile([P, W2], F32, name="t_mid0")
+            nc.vector.tensor_add(out=t_mid0[:], in0=lo, in1=size[:])
+            t_mid = keep.tile([P, W2], F32, name="t_mid")
+            nc.vector.tensor_tensor(out=t_mid[:], in0=t_mid0[:], in1=t_last[:], op=ALU.min)
+
+            zr_i = keep.tile([P, W2], I32, name="zr_i")
+            nc.gpsimd.iota(
+                zr_i[:], pattern=[[0, 4], [1, 16], [0, 2]], base=ZERO_ROW, channel_multiplier=0
+            )
+            zr = keep.tile([P, W2], F32, name="zr")
+            nc.vector.tensor_copy(out=zr[:], in_=zr_i[:])
+            st_i = keep.tile([P, W2], I32, name="st_i")
+            nc.gpsimd.iota(st_i[:], pattern=[[0, NN], [1, 2]], base=0, channel_multiplier=0)
+            st_f = keep.tile([P, W2], F32, name="st_f")
+            nc.vector.tensor_copy(out=st_f[:], in_=st_i[:])
+
+            rr = keep.tile([P, LOOKUPS, W2], F32, name="rr")
+            for a, t_ap in enumerate((lo, t_mid[:], t_last[:])):
+                nc.vector.tensor_add(out=rr[:, a, :], in0=roff[:], in1=t_ap)
+            r1 = keep.tile([P, LOOKUPS, W2], F32, name="r1")
+            nc.vector.tensor_tensor(out=r1[:], in0=rr[:], in1=over_lookups(zr[:]), op=ALU.subtract)
+            r2 = keep.tile([P, LOOKUPS, W2], F32, name="r2")
+            nc.vector.tensor_tensor(out=r2[:], in0=r1[:], in1=over_lookups(ne[:]), op=ALU.mult)
+            r3 = keep.tile([P, LOOKUPS, W2], F32, name="r3")
+            nc.vector.tensor_tensor(out=r3[:], in0=r2[:], in1=over_lookups(zr[:]), op=ALU.add)
+            ri = keep.tile([P, LOOKUPS, W2], I32, name="ri")
+            nc.vector.tensor_copy(out=ri[:], in_=r3[:])
+            rlo_i = keep.tile([P, LOOKUPS, W2], I32, name="rlo_i")
+            nc.vector.tensor_single_scalar(out=rlo_i[:], in_=ri[:], scalar=P - 1, op=ALU.bitwise_and)
+            rhi_i = keep.tile([P, LOOKUPS, W2], I32, name="rhi_i")
+            nc.vector.tensor_single_scalar(
+                out=rhi_i[:], in_=ri[:], scalar=7, op=ALU.logical_shift_right
+            )
+            rlo = keep.tile([P, LOOKUPS, W2], F32, name="rlo")
+            nc.vector.tensor_copy(out=rlo[:], in_=rlo_i[:])
+            rhi = keep.tile([P, LOOKUPS, W2], F32, name="rhi")
+            nc.vector.tensor_copy(out=rhi[:], in_=rhi_i[:])
+            x2 = keep.tile([P, LOOKUPS, W2], F32, name="x2")
+            nc.vector.scalar_tensor_tensor(
+                out=x2[:].rearrange("p a w -> p (a w)"),
+                in0=rlo[:].rearrange("p a w -> p (a w)"),
+                scalar=float(2 * CHUNKS),
+                in1=rhi[:].rearrange("p a w -> p (a w)"),
+                op0=ALU.mult,
+                op1=ALU.add,
+            )
+            x3 = keep.tile([P, LOOKUPS, W2], F32, name="x3")
+            nc.vector.tensor_add(out=x3[:], in0=x2[:], in1=rhi[:])
+            x4 = keep.tile([P, LOOKUPS, W2], F32, name="x4")
+            nc.vector.tensor_tensor(out=x4[:], in0=x3[:], in1=over_lookups(st_f[:]), op=ALU.add)
+
+            pidx = psum.tile([P, LOOKUPS, P], F32, tag="tp", bufs=TPB, name="pidx")
+            for a in range(LOOKUPS):
+                nc.tensor.transpose(pidx[:, a, :], x4[:, a, :], ident_f[:])
+            idx_i = keep.tile([P, LOOKUPS, NB], I32, name="idx_i")
+            for j in range(SLOTS):
+                nc.vector.tensor_scalar(
+                    out=idx_i[:, :, j:NB:SLOTS],
+                    in0=pidx[:, :, j:NB:SLOTS],
+                    scalar1=float(SLOT_ROWS * j),
+                    scalar2=None,
+                    op0=ALU.add,
+                )
+            made["idx_i"] = idx_i
+
+        def prep_weights():
+            wg = keep.tile([P, 4, P, 4], BF16, name="wg", align_bytes=64)
+            wg_f = (
+                wg[:]
+                .rearrange("p j m t -> p (j m t)")
+                .bitcast(F32)
+                .rearrange("p (j m u) -> p j m u", j=4, u=2)
+            )
+            for jj in range(2):
+                pw = psum.tile([P, 2, 2, P], F32, tag="tp", bufs=TPB, name="pw")
+                for jl in range(2):
+                    w_words = w_sb[:, 2 * jj + jl, :].bitcast(F32)
+                    for u in range(2):
+                        nc.tensor.transpose(
+                            pw[:, jl, u, :], w_words[:, P * u:P * u + P], ident_f[:]
+                        )
+                nc.vector.tensor_copy(
+                    out=wg_f[:, 2 * jj:2 * jj + 2, :, :], in_=pw[:].rearrange("p j u m -> p j m u")
+                )
+            wq = keep.tile([P, 512], U32, name="wq", align_bytes=64)
+            ws = keep.tile([P, 512], U8, name="ws", align_bytes=64)
+            nc.vector.quantize_mx(
+                out=wq[:].bitcast(FP8X4), scales=ws[:], in_=wg[:].rearrange("p j m t -> p (j m t)")
+            )
+            beta = keep.tile([P, 4], F32, name="beta")
+            nc.vector.tensor_copy(out=beta[:], in_=pb_b[:])
+            gam = keep.tile([P, 4], F32, name="gam")
+            nc.vector.tensor_copy(out=gam[:], in_=pb_g[:])
+            bet2 = keep.tile([P, 4], F32, name="bet2")
+            nc.vector.tensor_copy(out=bet2[:], in_=pb_e[:])
+            beta64 = keep.tile([P, 4], F32, name="beta64")
+            nc.vector.tensor_scalar_mul(out=beta64[:], in0=beta[:], scalar1=float(NN))
+            gsum = keep.tile([P, 32], F32, name="gsum")
+            nc.vector.tensor_reduce(
+                out=gsum[:], in_=ident_f[:].rearrange("p (g d) -> p g d", d=4), axis=AX.X, op=ALU.add
+            )
+            bd = keep.tile([P, 32, 4], F32, name="bd")
+            nc.vector.tensor_scalar(
+                out=bd[:],
+                in0=gsum[:].unsqueeze(2).to_broadcast([P, 32, 4]),
+                scalar1=1.0 / 1024.0,
                 scalar2=None,
-                op0=ALU.add,
+                op0=ALU.mult,
             )
-
-        wg = keep.tile([P, 4, P, 4], BF16, name="wg", align_bytes=64)
-        wg_f = (
-            wg[:]
-            .rearrange("p j m t -> p (j m t)")
-            .bitcast(F32)
-            .rearrange("p (j m u) -> p j m u", j=4, u=2)
-        )
-        for jj in range(2):
-            pw = psum.tile([P, 2, 2, P], F32, tag="tp", bufs=TPB, name="pw")
-            for jl in range(2):
-                w_words = w_sb[:, 2 * jj + jl, :].bitcast(F32)
-                for u in range(2):
-                    nc.tensor.transpose(pw[:, jl, u, :], w_words[:, P * u:P * u + P], ident_f[:])
-            nc.vector.tensor_copy(
-                out=wg_f[:, 2 * jj:2 * jj + 2, :, :], in_=pw[:].rearrange("p j u m -> p j m u")
-            )
-        wq = keep.tile([P, 512], U32, name="wq", align_bytes=64)
-        ws = keep.tile([P, 512], U8, name="ws", align_bytes=64)
-        nc.vector.quantize_mx(
-            out=wq[:].bitcast(FP8X4), scales=ws[:], in_=wg[:].rearrange("p j m t -> p (j m t)")
-        )
-
-        beta = keep.tile([P, 4], F32, name="beta")
-        nc.vector.tensor_copy(out=beta[:], in_=pb_b[:])
-        gam = keep.tile([P, 4], F32, name="gam")
-        nc.vector.tensor_copy(out=gam[:], in_=pb_g[:])
-        bet2 = keep.tile([P, 4], F32, name="bet2")
-        nc.vector.tensor_copy(out=bet2[:], in_=pb_e[:])
-        beta64 = keep.tile([P, 4], F32, name="beta64")
-        nc.vector.tensor_scalar_mul(out=beta64[:], in0=beta[:], scalar1=float(NN))
-
-        gsum = keep.tile([P, 32], F32, name="gsum")
-        nc.vector.tensor_reduce(
-            out=gsum[:], in_=ident_f[:].rearrange("p (g d) -> p g d", d=4), axis=AX.X, op=ALU.add
-        )
-        bd = keep.tile([P, 32, 4], F32, name="bd")
-        nc.vector.tensor_scalar(
-            out=bd[:],
-            in0=gsum[:].unsqueeze(2).to_broadcast([P, 32, 4]),
-            scalar1=1.0 / 1024.0,
-            scalar2=None,
-            op0=ALU.mult,
-        )
-
-        res = keep.tile([P, NB, 4, NN], F32, name="res")
+            made["w"] = (wq, ws, beta, gam, bet2, beta64, bd)
 
         def shift(b):
             nc.scalar.copy(
@@ -318,6 +326,7 @@ def tile_coarsepyramid_pb_kernel(
         gathered = {}
 
         def gather(b):
+            idx_i = made["idx_i"]
             got = []
             for a in range(LOOKUPS):
                 g = gat.tile([P, 2 * P], BF16, tag="g%d" % a, name="g%d" % a)
@@ -333,6 +342,7 @@ def tile_coarsepyramid_pb_kernel(
         groups = {}
 
         def finish(b):
+            gi, bi, nb, b0 = group_of[b]
             g0, g1, g2 = gathered[b]
             pm0 = gat.tile([P, 2 * P], BF16, tag="pm0", name="pm0")
             nc.vector.tensor_tensor(out=pm0[:], in0=g0[:], in1=g1[:], op=ALU.max)
@@ -341,20 +351,20 @@ def tile_coarsepyramid_pb_kernel(
             pp = psum.tile([P, 2, P], BF16, tag="pp", name="pp")
             for e in range(2):
                 nc.tensor.transpose(pp[:, e, :], pm[:, P * e:P * e + P], ident_b[:])
-            if b % GB == 0:
-                groups[b // GB] = grpp.tile(
-                    [P, GB, NN, 4], BF16, tag="grp", name="grp", align_bytes=64
-                )
-            grp = groups[b // GB]
+            if bi == 0:
+                groups[gi] = grpp.tile([P, nb, NN, 4], BF16, tag="grp", name="grp", align_bytes=64)
             nc.scalar.copy(
-                out=grp[:, b % GB, :, :].rearrange("p n (s e) -> p n s e", e=2),
+                out=groups[gi][:, bi, :, :].rearrange("p n (s e) -> p n s e", e=2),
                 in_=pp[:].rearrange("p e (n s) -> p n s e", s=2),
             )
+            if bi == nb - 1:
+                conv_norm(gi, b0, nb)
 
-        def conv_norm(g):
-            grp = groups[g]
-            codes = grpp.tile([P, 512], U32, tag="codes", name="codes", align_bytes=64)
-            scl = grpp.tile([P, 512], U8, tag="scl", name="scl", align_bytes=64)
+        def conv_norm(gi, b0, nb):
+            wq, ws, beta, gam, bet2, beta64, bd = made["w"]
+            grp = groups[gi]
+            codes = grpp.tile([P, nb * NN], U32, tag="codes", name="codes", align_bytes=64)
+            scl = grpp.tile([P, nb * NN], U8, tag="scl", name="scl", align_bytes=64)
             nc.vector.quantize_mx(
                 out=codes[:].bitcast(FP8X4),
                 scales=scl[:],
@@ -362,7 +372,7 @@ def tile_coarsepyramid_pb_kernel(
             )
             ys = []
             for j in range(4):
-                y = psum.tile([P, GB, NN], F32, tag="tp", bufs=TPB, name="y%d" % j)
+                y = psum.tile([P, nb, NN], F32, tag="tp", bufs=TPB, name="y%d" % j)
                 nc.tensor.matmul_mx(
                     out=y[:].rearrange("p b n -> p (b n)"),
                     lhsT=wq[:, P * j:P * j + P].bitcast(FP8X4),
@@ -373,10 +383,10 @@ def tile_coarsepyramid_pb_kernel(
                     stop=True,
                 )
                 ys.append(y)
-            st = small.tile([P, 2, 4, GB], F32, tag="st", name="st")
+            st = small.tile([P, 2, 4, nb], F32, tag="st", name="st")
             for j in range(4):
                 nc.vector.tensor_reduce(out=st[:, 0, j, :], in_=ys[j][:], axis=AX.X, op=ALU.add)
-                sq = small.tile([P, GB, NN], F32, tag="sq", name="sq")
+                sq = small.tile([P, nb, NN], F32, tag="sq", name="sq")
                 nc.scalar.activation(
                     out=sq[:], in_=ys[j][:], func=ACT.Square, bias=beta[:, j:j + 1], scale=1.0
                 )
@@ -384,14 +394,14 @@ def tile_coarsepyramid_pb_kernel(
             nc.vector.tensor_tensor(
                 out=st[:, 0, :, :],
                 in0=st[:, 0, :, :],
-                in1=beta64[:].unsqueeze(2).to_broadcast([P, 4, GB]),
+                in1=beta64[:].unsqueeze(2).to_broadcast([P, 4, nb]),
                 op=ALU.add,
             )
-            stj = small.tile([P, 2, GB], F32, tag="stj", name="stj")
+            stj = small.tile([P, 2, nb], F32, tag="stj", name="stj")
             nc.vector.tensor_reduce(
                 out=stj[:], in_=st[:].rearrange("p a j b -> p a b j"), axis=AX.X, op=ALU.add
             )
-            mvp = psum.tile([P, 2, GB], F32, tag="mv", name="mvp")
+            mvp = psum.tile([P, 2, nb], F32, tag="mv", name="mvp")
             nc.tensor.matmul(
                 out=mvp[:].rearrange("p a b -> p (a b)"),
                 lhsT=bd[:].rearrange("p g d -> p (g d)"),
@@ -399,50 +409,56 @@ def tile_coarsepyramid_pb_kernel(
                 start=True,
                 stop=True,
             )
-            mv = small.tile([P, 2, GB], F32, tag="mvs", name="mv")
+            mv = small.tile([P, 2, nb], F32, tag="mvs", name="mv")
             nc.vector.tensor_copy(out=mv[:], in_=mvp[:])
-            msq = small.tile([P, GB], F32, tag="msq", name="msq")
+            msq = small.tile([P, nb], F32, tag="msq", name="msq")
             nc.vector.tensor_mul(out=msq[:], in0=mv[:, 0, :], in1=mv[:, 0, :])
-            var = small.tile([P, GB], F32, tag="var", name="var")
+            var = small.tile([P, nb], F32, tag="var", name="var")
             nc.vector.scalar_tensor_tensor(
                 out=var[:], in0=mv[:, 1, :], scalar=EPS, in1=msq[:], op0=ALU.add, op1=ALU.subtract
             )
-            std = small.tile([P, GB], F32, tag="std", name="std")
+            std = small.tile([P, nb], F32, tag="std", name="std")
             nc.scalar.activation(out=std[:], in_=var[:], func=ACT.Sqrt)
-            rstd = small.tile([P, GB], F32, tag="rstd", name="rstd")
+            rstd = small.tile([P, nb], F32, tag="rstd", name="rstd")
             nc.vector.reciprocal(out=rstd[:], in_=std[:])
-            sc = small.tile([P, 4, GB], F32, tag="sc", name="sc")
+            sc = small.tile([P, 4, nb], F32, tag="sc", name="sc")
             nc.vector.tensor_tensor(
                 out=sc[:],
-                in0=gam[:].unsqueeze(2).to_broadcast([P, 4, GB]),
-                in1=rstd[:].unsqueeze(1).to_broadcast([P, 4, GB]),
+                in0=gam[:].unsqueeze(2).to_broadcast([P, 4, nb]),
+                in1=rstd[:].unsqueeze(1).to_broadcast([P, 4, nb]),
                 op=ALU.mult,
             )
-            d1 = small.tile([P, 4, GB], F32, tag="d1", name="d1")
+            d1 = small.tile([P, 4, nb], F32, tag="d1", name="d1")
             nc.vector.tensor_tensor(
                 out=d1[:],
-                in0=beta[:].unsqueeze(2).to_broadcast([P, 4, GB]),
-                in1=mv[:, 0, :].unsqueeze(1).to_broadcast([P, 4, GB]),
+                in0=beta[:].unsqueeze(2).to_broadcast([P, 4, nb]),
+                in1=mv[:, 0, :].unsqueeze(1).to_broadcast([P, 4, nb]),
                 op=ALU.subtract,
             )
-            d2 = small.tile([P, 4, GB], F32, tag="d2", name="d2")
+            d2 = small.tile([P, 4, nb], F32, tag="d2", name="d2")
             nc.vector.tensor_mul(out=d2[:], in0=d1[:], in1=sc[:])
-            sh = small.tile([P, 4, GB], F32, tag="sh", name="sh")
+            sh = small.tile([P, 4, nb], F32, tag="sh", name="sh")
             nc.vector.tensor_tensor(
                 out=sh[:],
                 in0=d2[:],
-                in1=bet2[:].unsqueeze(2).to_broadcast([P, 4, GB]),
+                in1=bet2[:].unsqueeze(2).to_broadcast([P, 4, nb]),
                 op=ALU.add,
             )
             for j in range(4):
-                for bi in range(GB):
+                for bi in range(nb):
                     nc.scalar.activation(
-                        out=res[:, g * GB + bi, j, :],
+                        out=res[:, b0 + bi, j, :],
                         in_=ys[j][:, bi, :],
                         func=ACT.Relu,
                         bias=sh[:, j, bi:bi + 1],
                         scale=sc[:, j, bi:bi + 1],
                     )
+
+        def store_result(b0, nb):
+            nc.sync.dma_start(
+                out=out_final[:, b0:b0 + nb, :],
+                in_=res[:, b0:b0 + nb, :, :].rearrange("p b j n -> p b (j n)"),
+            )
 
         shift(0)
         for i in range(NB + 4):
@@ -452,19 +468,20 @@ def tile_coarsepyramid_pb_kernel(
                 shift(i + 1)
             if i < NB:
                 tables(i)
+            if i == 0:
+                prep_rows()
             if 0 <= i - 1 < NB:
                 flip(i - 1)
             if 0 <= i - 2 < NB:
                 gather(i - 2)
             if 0 <= i - 1 < NB:
                 store(i - 1)
+            if i == 2:
+                prep_weights()
             if 0 <= i - 4 < NB:
                 finish(i - 4)
-                if (i - 4) % GB == GB - 1:
-                    conv_norm((i - 4) // GB)
 
-        for g in range(NB // GB):
-            nc.sync.dma_start(
-                out=out_final[:, g * GB:(g + 1) * GB, :],
-                in_=res[:, g * GB:(g + 1) * GB, :, :].rearrange("p b j n -> p b (j n)"),
-            )
+        b0 = 0
+        for nb in GROUPS:
+            store_result(b0, nb)
+            b0 += nb

@@ -57,6 +57,7 @@ def tile_coarsepyramid_pb_kernel(
         grpp = ctx.enter_context(tc.tile_pool(name="grpp", bufs=2))
         small = ctx.enter_context(tc.tile_pool(name="small", bufs=2))
         psum = ctx.enter_context(tc.psum_pool(name="psum", bufs=1))
+        ctx.enter_context(tc.manual_schedule())
 
         out_flat = out.rearrange("b c n -> (b c n)")
         out_rows = out_flat.rearrange("(r w) -> r w", w=P)
@@ -468,15 +469,15 @@ def tile_coarsepyramid_pb_kernel(
                 shift(i + 1)
             if i < NB:
                 tables(i)
-            if i == 0:
-                prep_rows()
             if 0 <= i - 1 < NB:
                 flip(i - 1)
             if 0 <= i - 2 < NB:
                 gather(i - 2)
             if 0 <= i - 1 < NB:
                 store(i - 1)
-            if i == 2:
+            if i == 1:
+                prep_rows()
+            if i == 3:
                 prep_weights()
             if 0 <= i - 4 < NB:
                 finish(i - 4)

@@ -57,7 +57,6 @@ def tile_coarsepyramid_pb_kernel(
         grpp = ctx.enter_context(tc.tile_pool(name="grpp", bufs=2))
         small = ctx.enter_context(tc.tile_pool(name="small", bufs=2))
         psum = ctx.enter_context(tc.psum_pool(name="psum", bufs=1))
-        ctx.enter_context(tc.manual_schedule())
 
         out_flat = out.rearrange("b c n -> (b c n)")
         out_rows = out_flat.rearrange("(r w) -> r w", w=P)
@@ -73,40 +72,25 @@ def tile_coarsepyramid_pb_kernel(
             )
             frames[b] = x0
 
-        load(0)
         segb = keep.tile([P, 4 * NN], BF16, name="segb")
-        nc.vector.memset(segb[:], 0.0)
-        nc.sync.dma_start(out=segb[0:NB, :], in_=frame_segments.rearrange("b n f -> b (n f)"))
-        load(1)
-        load(2)
         w_sb = keep.tile([P, 4, 512], BF16, name="w_sb")
-        nc.sync.dma_start(out=w_sb[:], in_=w_roi.rearrange("(m j) c -> m j c", j=4))
         pb_b = keep.tile([P, 4], BF16, name="pb_b")
-        nc.sync.dma_start(out=pb_b[:], in_=b_roi.rearrange("(m j) -> m j", j=4))
         pb_g = keep.tile([P, 4], BF16, name="pb_g")
-        nc.sync.dma_start(out=pb_g[:], in_=g_roi.rearrange("(m j) -> m j", j=4))
         pb_e = keep.tile([P, 4], BF16, name="pb_e")
-        nc.sync.dma_start(out=pb_e[:], in_=be_roi.rearrange("(m j) -> m j", j=4))
-
         one = keep.tile([P, 1], F32, name="one")
-        nc.vector.memset(one[:], 1.0)
         one2 = keep.tile([P, 1], F32, name="one2")
-        nc.scalar.activation(out=one2[:], in_=one[:], func=ACT.Sqrt)
-
         ident_b = keep.tile([P, P], BF16, name="ident_b")
-        make_identity(nc, ident_b[:])
         ident_f = keep.tile([P, P], F32, name="ident_f")
-        make_identity(nc, ident_f[:])
-
         uppers = []
         shifted = []
         for i in range(NTAB):
-            x1 = keep.tile([P, 2, 2, NT], BF16, name="x1_%d" % i)
-            nc.vector.memset(x1[:], 0.0)
-            shifted.append(x1)
-            up = keep.tile([P, 2, 2, UPPER], BF16, name="up%d" % i)
-            nc.vector.memset(up[:, :, :, OZ:UPPER], 0.0)
-            uppers.append(up)
+            shifted.append(keep.tile([P, 2, 2, NT], BF16, name="x1_%d" % i))
+            uppers.append(keep.tile([P, 2, 2, UPPER], BF16, name="up%d" % i))
+
+        def clear(i):
+            nc.vector.memset(shifted[i][:], 0.0)
+            nc.vector.memset(uppers[i][:, :, :, OZ:UPPER], 0.0)
+
         tmp_a = keep.tile([P, 2, 2, NT], BF16, name="tmp_a")
         tmp_b = keep.tile([P, 2, 2, NT], BF16, name="tmp_b")
         res = keep.tile([P, NB, 4, NN], F32, name="res")
@@ -114,7 +98,7 @@ def tile_coarsepyramid_pb_kernel(
         def over_lookups(ap):
             return ap.unsqueeze(1).to_broadcast([P, LOOKUPS, W2])
 
-        def prep_rows():
+        def prep_rows_a():
             sf = keep.tile([P, 2 * W2], F32, name="sf")
             nc.vector.tensor_scalar(
                 out=sf[:], in0=segb[:], scalar1=0.0, scalar2=float(NT - 1), op0=ALU.max, op1=ALU.min
@@ -172,6 +156,10 @@ def tile_coarsepyramid_pb_kernel(
             st_f = keep.tile([P, W2], F32, name="st_f")
             nc.vector.tensor_copy(out=st_f[:], in_=st_i[:])
 
+            made["rows_a"] = (lo, t_mid, t_last, roff, zr, ne, st_f)
+
+        def prep_rows_b():
+            lo, t_mid, t_last, roff, zr, ne, st_f = made["rows_a"]
             rr = keep.tile([P, LOOKUPS, W2], F32, name="rr")
             for a, t_ap in enumerate((lo, t_mid[:], t_last[:])):
                 nc.vector.tensor_add(out=rr[:, a, :], in0=roff[:], in1=t_ap)
@@ -461,23 +449,46 @@ def tile_coarsepyramid_pb_kernel(
                 in_=res[:, b0:b0 + nb, :, :].rearrange("p b j n -> p b (j n)"),
             )
 
-        shift(0)
+        with tc.manual_schedule():
+            load(0)
+            nc.vector.memset(segb[:], 0.0)
+            nc.sync.dma_start(
+                out=segb[0:NB, :], in_=frame_segments.rearrange("b n f -> b (n f)")
+            )
+            load(1)
+            load(2)
+            nc.sync.dma_start(out=w_sb[:], in_=w_roi.rearrange("(m j) c -> m j c", j=4))
+            nc.sync.dma_start(out=pb_b[:], in_=b_roi.rearrange("(m j) -> m j", j=4))
+            nc.sync.dma_start(out=pb_g[:], in_=g_roi.rearrange("(m j) -> m j", j=4))
+            nc.sync.dma_start(out=pb_e[:], in_=be_roi.rearrange("(m j) -> m j", j=4))
+            nc.vector.memset(one[:], 1.0)
+            nc.scalar.activation(out=one2[:], in_=one[:], func=ACT.Sqrt)
+            make_identity(nc, ident_b[:])
+            make_identity(nc, ident_f[:])
+            clear(0)
+            shift(0)
+            prep_rows_a()
+            tables(0)
+            flip(0)
+            store(0)
+            clear(1)
+            clear(2)
+            prep_rows_b()
+
         for i in range(NB + 4):
             if 3 <= i + 3 < NB:
                 load(i + 3)
             if 1 <= i + 1 < NB:
                 shift(i + 1)
-            if i < NB:
+            if 1 <= i < NB:
                 tables(i)
-            if 0 <= i - 1 < NB:
+            if 1 <= i - 1 < NB:
                 flip(i - 1)
             if 0 <= i - 2 < NB:
                 gather(i - 2)
-            if 0 <= i - 1 < NB:
+            if 1 <= i - 1 < NB:
                 store(i - 1)
-            if i == 1:
-                prep_rows()
-            if i == 3:
+            if i == 2:
                 prep_weights()
             if 0 <= i - 4 < NB:
                 finish(i - 4)

from contextlib import ExitStack

import concourse.bass as bass
import concourse.mybir as mybir
from concourse.masks import make_identity

F32 = mybir.dt.float32
BF16 = mybir.dt.bfloat16
I32 = mybir.dt.int32
U32 = mybir.dt.uint32
U8 = mybir.dt.uint8
FP8X4 = mybir.dt.float8_e4m3fn_x4
ALU = mybir.AluOpType
ACT = mybir.ActivationFunctionType
AX = mybir.AxisListType

P = 128
NB = 48
NT = 256
NN = 64
W2 = 2 * NN
LOOKUPS = 3
THRESH = (4.0, 12.0, 36.0, 108.0)
SIZE_STEP = (3.0, 8.0, 24.0, 72.0)
ROW_STEP = (256.0, 254.0, 246.0, 222.0)
O1, O2, O3, O4, OZ = 0, 254, 500, 722, 872
UPPER = 896
ZERO_ROW = NT + OZ
CHUNKS = 9
SLOTS = 5
SLOT_ROWS = 2 * CHUNKS * P
SLOT_WORDS = SLOT_ROWS * P
NTAB = 3
TPB = 6
GROUPS = (8, 8, 8, 8, 8, 4, 2, 2)
EPS = 1e-5

FLOPS = 2 * 48 * 512 * 512 * 64


def tile_coarsepyramid_pb_kernel(
    tc, frame_level_feature, frame_segments, w_roi, b_roi, g_roi, be_roi, out
):
    nc = tc.nc
    group_of = {}
    b_first = 0
    for gi, nb in enumerate(GROUPS):
        for bi in range(nb):
            group_of[b_first + bi] = (gi, bi, nb, b_first)
        b_first += nb

    with ExitStack() as ctx:
        keep = ctx.enter_context(tc.tile_pool(name="keep", bufs=1))
        xin = ctx.enter_context(tc.tile_pool(name="xin", bufs=6))
        stage = ctx.enter_context(tc.tile_pool(name="stage", bufs=5))
        gat = ctx.enter_context(tc.tile_pool(name="gat", bufs=6))
        grpp = ctx.enter_context(tc.tile_pool(name="grpp", bufs=2))
        small = ctx.enter_context(tc.tile_pool(name="small", bufs=2))
        psum = ctx.enter_context(tc.psum_pool(name="psum", bufs=1))

        out_flat = out.rearrange("b c n -> (b c n)")
        out_rows = out_flat.rearrange("(r w) -> r w", w=P)
        out_final = out.rearrange("b (m j) n -> m b (j n)", j=4)

        made = {}
        frames = {}

        def load(b):
            x0 = xin.tile([P, 2, 2, NT], BF16, tag="x0", name="x0")
            nc.sync.dma_start(
                out=x0[:], in_=frame_level_feature[b].rearrange("(s p e) t -> p s e t", s=2, e=2)
            )
            frames[b] = x0

        segb = keep.tile([P, 4 * NN], BF16, name="segb")
        w_sb = keep.tile([P, 4, 512], BF16, name="w_sb")
        pb_b = keep.tile([P, 4], BF16, name="pb_b")
        pb_g = keep.tile([P, 4], BF16, name="pb_g")
        pb_e = keep.tile([P, 4], BF16, name="pb_e")
        one = keep.tile([P, 1], F32, name="one")
        one2 = keep.tile([P, 1], F32, name="one2")
        ident_b = keep.tile([P, P], BF16, name="ident_b")
        ident_f = keep.tile([P, P], F32, name="ident_f")
        uppers = []
        shifted = []
        for i in range(NTAB):
            shifted.append(keep.tile([P, 2, 2, NT], BF16, name="x1_%d" % i))
            uppers.append(keep.tile([P, 2, 2, UPPER], BF16, name="up%d" % i))

        def clear(i):
            nc.vector.memset(shifted[i][:], 0.0)
            nc.vector.memset(uppers[i][:, :, :, OZ:UPPER], 0.0)

        tmp_a = keep.tile([P, 2, 2, NT], BF16, name="tmp_a")
        tmp_b = keep.tile([P, 2, 2, NT], BF16, name="tmp_b")
        res = keep.tile([P, NB, 4, NN], F32, name="res")

        def over_lookups(ap):
            return ap.unsqueeze(1).to_broadcast([P, LOOKUPS, W2])

        def prep_rows_a():
            sf = keep.tile([P, 2 * W2], F32, name="sf")
            nc.vector.tensor_scalar(
                out=sf[:], in0=segb[:], scalar1=0.0, scalar2=float(NT - 1), op0=ALU.max, op1=ALU.min
            )
            si = keep.tile([P, 2 * W2], I32, name="si")
            nc.vector.tensor_copy(out=si[:], in_=sf[:])
            fi = keep.tile([P, 2 * W2], F32, name="fi")
            nc.vector.tensor_copy(out=fi[:], in_=si[:])
            gt = keep.tile([P, 2 * W2], F32, name="gt")
            nc.vector.tensor_tensor(out=gt[:], in0=fi[:], in1=sf[:], op=ALU.is_gt)
            fl = keep.tile([P, 2 * W2], F32, name="fl")
            nc.vector.tensor_sub(out=fl[:], in0=fi[:], in1=gt[:])
            fl2 = fl[:].rearrange("p (w e) -> p w e", e=2)
            lo = fl2[:, :, 0]
            hi = fl2[:, :, 1]

            ld = keep.tile([P, W2], F32, name="ld")
            nc.vector.tensor_sub(out=ld[:], in0=hi, in1=lo)
            ne = keep.tile([P, W2], F32, name="ne")
            nc.vector.tensor_single_scalar(out=ne[:], in_=ld[:], scalar=0.0, op=ALU.is_ge)
            lc = keep.tile([P, W2], F32, name="lc")
            nc.vector.tensor_scalar(
                out=lc[:], in0=ld[:], scalar1=0.0, scalar2=1.0, op0=ALU.max, op1=ALU.add
            )
            size = keep.tile([P, W2], F32, name="size")
            nc.vector.memset(size[:], 1.0)
            roff = keep.tile([P, W2], F32, name="roff")
            nc.vector.memset(roff[:], 0.0)
            for j in range(4):
                cj = keep.tile([P, W2], F32, name="cj%d" % j)
                nc.vector.tensor_single_scalar(out=cj[:], in_=lc[:], scalar=THRESH[j], op=ALU.is_ge)
                nc.vector.scalar_tensor_tensor(
                    out=size[:], in0=cj[:], scalar=SIZE_STEP[j], in1=size[:], op0=ALU.mult, op1=ALU.add
                )
                nc.vector.scalar_tensor_tensor(
                    out=roff[:], in0=cj[:], scalar=ROW_STEP[j], in1=roff[:], op0=ALU.mult, op1=ALU.add
                )
            t_last0 = keep.tile([P, W2], F32, name="t_last0")
            nc.vector.tensor_sub(out=t_last0[:], in0=hi, in1=size[:])
            t_last = keep.tile([P, W2], F32, name="t_last")
            nc.vector.tensor_scalar_add(out=t_last[:], in0=t_last0[:], scalar1=1.0)
            t_mid0 = keep.tile([P, W2], F32, name="t_mid0")
            nc.vector.tensor_add(out=t_mid0[:], in0=lo, in1=size[:])
            t_mid = keep.tile([P, W2], F32, name="t_mid")
            nc.vector.tensor_tensor(out=t_mid[:], in0=t_mid0[:], in1=t_last[:], op=ALU.min)

            zr_i = keep.tile([P, W2], I32, name="zr_i")
            nc.gpsimd.iota(
                zr_i[:], pattern=[[0, 4], [1, 16], [0, 2]], base=ZERO_ROW, channel_multiplier=0
            )
            zr = keep.tile([P, W2], F32, name="zr")
            nc.vector.tensor_copy(out=zr[:], in_=zr_i[:])
            st_i = keep.tile([P, W2], I32, name="st_i")
            nc.gpsimd.iota(st_i[:], pattern=[[0, NN], [1, 2]], base=0, channel_multiplier=0)
            st_f = keep.tile([P, W2], F32, name="st_f")
            nc.vector.tensor_copy(out=st_f[:], in_=st_i[:])

            made["rows_a"] = (lo, t_mid, t_last, roff, zr, ne, st_f)

        def prep_rows_b():
            lo, t_mid, t_last, roff, zr, ne, st_f = made["rows_a"]
            rr = keep.tile([P, LOOKUPS, W2], F32, name="rr")
            for a, t_ap in enumerate((lo, t_mid[:], t_last[:])):
                nc.vector.tensor_add(out=rr[:, a, :], in0=roff[:], in1=t_ap)
            r1 = keep.tile([P, LOOKUPS, W2], F32, name="r1")
            nc.vector.tensor_tensor(out=r1[:], in0=rr[:], in1=over_lookups(zr[:]), op=ALU.subtract)
            r2 = keep.tile([P, LOOKUPS, W2], F32, name="r2")
            nc.vector.tensor_tensor(out=r2[:], in0=r1[:], in1=over_lookups(ne[:]), op=ALU.mult)
            r3 = keep.tile([P, LOOKUPS, W2], F32, name="r3")
            nc.vector.tensor_tensor(out=r3[:], in0=r2[:], in1=over_lookups(zr[:]), op=ALU.add)
            ri = keep.tile([P, LOOKUPS, W2], I32, name="ri")
            nc.vector.tensor_copy(out=ri[:], in_=r3[:])
            rlo_i = keep.tile([P, LOOKUPS, W2], I32, name="rlo_i")
            nc.vector.tensor_single_scalar(out=rlo_i[:], in_=ri[:], scalar=P - 1, op=ALU.bitwise_and)
            rhi_i = keep.tile([P, LOOKUPS, W2], I32, name="rhi_i")
            nc.vector.tensor_single_scalar(
                out=rhi_i[:], in_=ri[:], scalar=7, op=ALU.logical_shift_right
            )
            rlo = keep.tile([P, LOOKUPS, W2], F32, name="rlo")
            nc.vector.tensor_copy(out=rlo[:], in_=rlo_i[:])
            rhi = keep.tile([P, LOOKUPS, W2], F32, name="rhi")
            nc.vector.tensor_copy(out=rhi[:], in_=rhi_i[:])
            x2 = keep.tile([P, LOOKUPS, W2], F32, name="x2")
            nc.vector.scalar_tensor_tensor(
                out=x2[:].rearrange("p a w -> p (a w)"),
                in0=rlo[:].rearrange("p a w -> p (a w)"),
                scalar=float(2 * CHUNKS),
                in1=rhi[:].rearrange("p a w -> p (a w)"),
                op0=ALU.mult,
                op1=ALU.add,
            )
            x3 = keep.tile([P, LOOKUPS, W2], F32, name="x3")
            nc.vector.tensor_add(out=x3[:], in0=x2[:], in1=rhi[:])
            x4 = keep.tile([P, LOOKUPS, W2], F32, name="x4")
            nc.vector.tensor_tensor(out=x4[:], in0=x3[:], in1=over_lookups(st_f[:]), op=ALU.add)

            pidx = psum.tile([P, LOOKUPS, P], F32, tag="tp", bufs=TPB, name="pidx")
            for a in range(LOOKUPS):
                nc.tensor.transpose(pidx[:, a, :], x4[:, a, :], ident_f[:])
            idx_i = keep.tile([P, LOOKUPS, NB], I32, name="idx_i")
            for j in range(SLOTS):
                nc.vector.tensor_scalar(
                    out=idx_i[:, :, j:NB:SLOTS],
                    in0=pidx[:, :, j:NB:SLOTS],
                    scalar1=float(SLOT_ROWS * j),
                    scalar2=None,
                    op0=ALU.add,
                )
            made["idx_i"] = idx_i

        def prep_weights():
            wg = keep.tile([P, 4, P, 4], BF16, name="wg", align_bytes=64)
            wg_f = (
                wg[:]
                .rearrange("p j m t -> p (j m t)")
                .bitcast(F32)
                .rearrange("p (j m u) -> p j m u", j=4, u=2)
            )
            for jj in range(2):
                pw = psum.tile([P, 2, 2, P], F32, tag="tp", bufs=TPB, name="pw")
                for jl in range(2):
                    w_words = w_sb[:, 2 * jj + jl, :].bitcast(F32)
                    for u in range(2):
                        nc.tensor.transpose(
                            pw[:, jl, u, :], w_words[:, P * u:P * u + P], ident_f[:]
                        )
                nc.vector.tensor_copy(
                    out=wg_f[:, 2 * jj:2 * jj + 2, :, :], in_=pw[:].rearrange("p j u m -> p j m u")
                )
            wq = keep.tile([P, 512], U32, name="wq", align_bytes=64)
            ws = keep.tile([P, 512], U8, name="ws", align_bytes=64)
            nc.vector.quantize_mx(
                out=wq[:].bitcast(FP8X4), scales=ws[:], in_=wg[:].rearrange("p j m t -> p (j m t)")
            )
            beta = keep.tile([P, 4], F32, name="beta")
            nc.vector.tensor_copy(out=beta[:], in_=pb_b[:])
            gam = keep.tile([P, 4], F32, name="gam")
            nc.vector.tensor_copy(out=gam[:], in_=pb_g[:])
            bet2 = keep.tile([P, 4], F32, name="bet2")
            nc.vector.tensor_copy(out=bet2[:], in_=pb_e[:])
            beta64 = keep.tile([P, 4], F32, name="beta64")
            nc.vector.tensor_scalar_mul(out=beta64[:], in0=beta[:], scalar1=float(NN))
            gsum = keep.tile([P, 32], F32, name="gsum")
            nc.vector.tensor_reduce(
                out=gsum[:], in_=ident_f[:].rearrange("p (g d) -> p g d", d=4), axis=AX.X, op=ALU.add
            )
            bd = keep.tile([P, 32, 4], F32, name="bd")
            nc.vector.tensor_scalar(
                out=bd[:],
                in0=gsum[:].unsqueeze(2).to_broadcast([P, 32, 4]),
                scalar1=1.0 / 1024.0,
                scalar2=None,
                op0=ALU.mult,
            )
            made["w"] = (wq, ws, beta, gam, bet2, beta64, bd)

        def shift(b):
            nc.scalar.copy(
                out=shifted[b % NTAB][:, :, :, 0:NT - 1], in_=frames[b][:, :, :, 1:NT]
            )

        def vmax(dst, d0, src0, a0, src1, b0, n):
            nc.vector.tensor_tensor(
                out=dst[:, :, :, d0:d0 + n],
                in0=src0[:, :, :, a0:a0 + n],
                in1=src1[:, :, :, b0:b0 + n],
                op=ALU.max,
            )

        def tables(b):
            x0 = frames[b]
            up = uppers[b % NTAB]
            vmax(tmp_a, 0, x0, 0, shifted[b % NTAB], 0, 256)
            vmax(up, O1, tmp_a, 0, tmp_a, 2, 254)
            vmax(tmp_b, 0, up, O1, up, O1 + 4, 250)
            vmax(up, O2, tmp_b, 0, up, O1 + 8, 246)
            vmax(tmp_a, 0, up, O2, up, O2 + 12, 234)
            vmax(up, O3, tmp_a, 0, up, O2 + 24, 222)
            vmax(tmp_b, 0, up, O3, up, O3 + 36, 186)
            vmax(up, O4, tmp_b, 0, up, O3 + 72, 150)

        staged = {}

        def flip(b):
            x0 = frames[b]
            up = uppers[b % NTAB]
            stg = stage.tile([P, CHUNKS * 4 * P], BF16, tag="stg", name="stg")
            stg_f = stg[:].bitcast(F32)
            for q0 in range(0, CHUNKS, 2):
                nq = min(2, CHUNKS - q0)
                pt = psum.tile([P, 8 * P], BF16, tag="tp", bufs=TPB, name="pt")
                for qi in range(nq):
                    q = q0 + qi
                    for s in range(2):
                        for e in range(2):
                            c0 = ((qi * 2 + s) * 2 + e) * P
                            if q < 2:
                                src = x0[:, s, e, P * q:P * q + P]
                            else:
                                src = up[:, s, e, P * (q - 2):P * (q - 2) + P]
                            nc.tensor.transpose(pt[:, c0:c0 + P], src, ident_b[:])
                nc.scalar.copy(
                    out=stg_f[:, 2 * P * q0:2 * P * (q0 + nq)],
                    in_=pt[:].bitcast(F32)[:, 0:2 * P * nq],
                )
            staged[b] = stg_f

        def store(b):
            w0 = (b % SLOTS) * SLOT_WORDS
            nc.sync.dma_start(
                out=out_flat[w0:w0 + SLOT_WORDS].rearrange("(p w) -> p w", p=P), in_=staged[b]
            )

        gathered = {}

        def gather(b):
            idx_i = made["idx_i"]
            got = []
            for a in range(LOOKUPS):
                g = gat.tile([P, 2 * P], BF16, tag="g%d" % a, name="g%d" % a)
                nc.gpsimd.indirect_dma_start(
                    out=g[:].bitcast(F32),
                    out_offset=None,
                    in_=out_rows[0:(b % SLOTS + 1) * SLOT_ROWS, :],
                    in_offset=bass.IndirectOffsetOnAxis(ap=idx_i[:, a, b:b + 1], axis=0),
                )
                got.append(g)
            gathered[b] = got

        groups = {}

        def finish(b):
            gi, bi, nb, b0 = group_of[b]
            g0, g1, g2 = gathered[b]
            pm0 = gat.tile([P, 2 * P], BF16, tag="pm0", name="pm0")
            nc.vector.tensor_tensor(out=pm0[:], in0=g0[:], in1=g1[:], op=ALU.max)
            pm = gat.tile([P, 2 * P], BF16, tag="pm", name="pm")
            nc.vector.tensor_tensor(out=pm[:], in0=pm0[:], in1=g2[:], op=ALU.max)
            pp = psum.tile([P, 2, P], BF16, tag="pp", name="pp")
            for e in range(2):
                nc.tensor.transpose(pp[:, e, :], pm[:, P * e:P * e + P], ident_b[:])
            if bi == 0:
                groups[gi] = grpp.tile([P, nb, NN, 4], BF16, tag="grp", name="grp", align_bytes=64)
            nc.scalar.copy(
                out=groups[gi][:, bi, :, :].rearrange("p n (s e) -> p n s e", e=2),
                in_=pp[:].rearrange("p e (n s) -> p n s e", s=2),
            )
            if bi == nb - 1:
                conv_norm(gi, b0, nb)

        def conv_norm(gi, b0, nb):
            wq, ws, beta, gam, bet2, beta64, bd = made["w"]
            grp = groups[gi]
            codes = grpp.tile([P, nb * NN], U32, tag="codes", name="codes", align_bytes=64)
            scl = grpp.tile([P, nb * NN], U8, tag="scl", name="scl", align_bytes=64)
            nc.vector.quantize_mx(
                out=codes[:].bitcast(FP8X4),
                scales=scl[:],
                in_=grp[:].rearrange("p b n t -> p (b n t)"),
            )
            ys = []
            for j in range(4):
                y = psum.tile([P, nb, NN], F32, tag="tp", bufs=TPB, name="y%d" % j)
                nc.tensor.matmul_mx(
                    out=y[:].rearrange("p b n -> p (b n)"),
                    lhsT=wq[:, P * j:P * j + P].bitcast(FP8X4),
                    lhsT_scale=ws[:, P * j:P * j + P],
                    rhs=codes[:].bitcast(FP8X4),
                    rhs_scale=scl[:],
                    start=True,
                    stop=True,
                )
                ys.append(y)
            st = small.tile([P, 2, 4, nb], F32, tag="st", name="st")
            for j in range(4):
                nc.vector.tensor_reduce(out=st[:, 0, j, :], in_=ys[j][:], axis=AX.X, op=ALU.add)
                sq = small.tile([P, nb, NN], F32, tag="sq", name="sq")
                nc.scalar.activation(
                    out=sq[:], in_=ys[j][:], func=ACT.Square, bias=beta[:, j:j + 1], scale=1.0
                )
                nc.vector.tensor_reduce(out=st[:, 1, j, :], in_=sq[:], axis=AX.X, op=ALU.add)
            nc.vector.tensor_tensor(
                out=st[:, 0, :, :],
                in0=st[:, 0, :, :],
                in1=beta64[:].unsqueeze(2).to_broadcast([P, 4, nb]),
                op=ALU.add,
            )
            stj = small.tile([P, 2, nb], F32, tag="stj", name="stj")
            nc.vector.tensor_reduce(
                out=stj[:], in_=st[:].rearrange("p a j b -> p a b j"), axis=AX.X, op=ALU.add
            )
            mvp = psum.tile([P, 2, nb], F32, tag="mv", name="mvp")
            nc.tensor.matmul(
                out=mvp[:].rearrange("p a b -> p (a b)"),
                lhsT=bd[:].rearrange("p g d -> p (g d)"),
                rhs=stj[:].rearrange("p a b -> p (a b)"),
                start=True,
                stop=True,
            )
            mv = small.tile([P, 2, nb], F32, tag="mvs", name="mv")
            nc.vector.tensor_copy(out=mv[:], in_=mvp[:])
            msq = small.tile([P, nb], F32, tag="msq", name="msq")
            nc.vector.tensor_mul(out=msq[:], in0=mv[:, 0, :], in1=mv[:, 0, :])
            var = small.tile([P, nb], F32, tag="var", name="var")
            nc.vector.scalar_tensor_tensor(
                out=var[:], in0=mv[:, 1, :], scalar=EPS, in1=msq[:], op0=ALU.add, op1=ALU.subtract
            )
            std = small.tile([P, nb], F32, tag="std", name="std")
            nc.scalar.activation(out=std[:], in_=var[:], func=ACT.Sqrt)
            rstd = small.tile([P, nb], F32, tag="rstd", name="rstd")
            nc.vector.reciprocal(out=rstd[:], in_=std[:])
            sc = small.tile([P, 4, nb], F32, tag="sc", name="sc")
            nc.vector.tensor_tensor(
                out=sc[:],
                in0=gam[:].unsqueeze(2).to_broadcast([P, 4, nb]),
                in1=rstd[:].unsqueeze(1).to_broadcast([P, 4, nb]),
                op=ALU.mult,
            )
            d1 = small.tile([P, 4, nb], F32, tag="d1", name="d1")
            nc.vector.tensor_tensor(
                out=d1[:],
                in0=beta[:].unsqueeze(2).to_broadcast([P, 4, nb]),
                in1=mv[:, 0, :].unsqueeze(1).to_broadcast([P, 4, nb]),
                op=ALU.subtract,
            )
            d2 = small.tile([P, 4, nb], F32, tag="d2", name="d2")
            nc.vector.tensor_mul(out=d2[:], in0=d1[:], in1=sc[:])
            sh = small.tile([P, 4, nb], F32, tag="sh", name="sh")
            nc.vector.tensor_tensor(
                out=sh[:],
                in0=d2[:],
                in1=bet2[:].unsqueeze(2).to_broadcast([P, 4, nb]),
                op=ALU.add,
            )
            for j in range(4):
                for bi in range(nb):
                    nc.scalar.activation(
                        out=res[:, b0 + bi, j, :],
                        in_=ys[j][:, bi, :],
                        func=ACT.Relu,
                        bias=sh[:, j, bi:bi + 1],
                        scale=sc[:, j, bi:bi + 1],
                    )

        def store_result(b0, nb):
            nc.sync.dma_start(
                out=out_final[:, b0:b0 + nb, :],
                in_=res[:, b0:b0 + nb, :, :].rearrange("p b j n -> p b (j n)"),
            )

        with tc.manual_schedule():
            load(0)
            nc.vector.memset(segb[:], 0.0)
            nc.sync.dma_start(
                out=segb[0:NB, :], in_=frame_segments.rearrange("b n f -> b (n f)")
            )
            load(1)
            load(2)
            nc.sync.dma_start(out=w_sb[:], in_=w_roi.rearrange("(m j) c -> m j c", j=4))
            nc.sync.dma_start(out=pb_b[:], in_=b_roi.rearrange("(m j) -> m j", j=4))
            nc.sync.dma_start(out=pb_g[:], in_=g_roi.rearrange("(m j) -> m j", j=4))
            nc.sync.dma_start(out=pb_e[:], in_=be_roi.rearrange("(m j) -> m j", j=4))
            nc.vector.memset(one[:], 1.0)
            nc.scalar.activation(out=one2[:], in_=one[:], func=ACT.Sqrt)
            make_identity(nc, ident_b[:])
            make_identity(nc, ident_f[:])
            clear(0)
            shift(0)
            prep_rows_a()
            tables(0)
            flip(0)
            store(0)
            clear(1)
            clear(2)
            prep_rows_b()

        for i in range(NB + 4):
            if 3 <= i + 3 < NB:
                load(i + 3)
            if 1 <= i + 1 < NB:
                shift(i + 1)
            if 1 <= i < NB:
                tables(i)
            if 1 <= i - 1 < NB:
                flip(i - 1)
            if 0 <= i - 2 < NB:
                gather(i - 2)
            if 1 <= i - 1 < NB:
                store(i - 1)
            if i == 2:
                prep_weights()
            if 0 <= i - 4 < NB:
                finish(i - 4)

        b0 = 0
        for nb in GROUPS:
            store_result(b0, nb)
            b0 += nb
